import numpy as np
import ml_dtypes


def mxq(x, axis, fmt="e4m3"):
    dtype, down = {"e4m3": (ml_dtypes.float8_e4m3fn, 7), "e5m2": (ml_dtypes.float8_e5m2, 14)}[fmt]
    v = np.moveaxis(np.asarray(x, np.float32).astype(ml_dtypes.bfloat16).astype(np.float64), axis, -1)
    blocks = v.reshape(v.shape[:-1] + (-1, 32))
    amax = np.abs(blocks).max(-1, keepdims=True)
    byte = np.maximum(np.where(amax > 0, np.frexp(amax)[1] - 1 + 127, 0) - down, 1)
    scale = np.exp2(byte - 127.0)
    codes = (blocks / scale).astype(np.float32).astype(dtype).astype(np.float64)
    return np.moveaxis((codes * scale).reshape(v.shape), -1, axis)


WIDE = False


def mx_kscale(k):
    if not WIDE:
        return np.ones(k)
    levels = np.array([10, -10, 5, -5, 0])
    a = np.random.permutation(np.resize(levels, k // 512 * 4)).reshape(k // 512, 4)
    idx = np.arange(k)
    return np.exp2(a[idx // 512, idx % 128 // 32])


BF16 = ml_dtypes.bfloat16


def bf(x):
    return np.asarray(x, np.float32).astype(BF16)


def f64(x):
    return np.asarray(x).astype(np.float64)


G, NSPIN, D_ONE, D_TWO = 64, 4, 256, 128
N = 2 * G * NSPIN
K1 = D_ONE + 2 * D_TWO
K2 = 2 * D_ONE
TANH_GAIN = 1.5927812698663606


def setup_inputs():
    s = mx_kscale(K1)[D_ONE:]
    w1 = np.random.standard_normal((K1, D_ONE)) / np.sqrt(K1)
    w1[D_ONE:] = w1[D_ONE:] / s[:, None]
    return {"h_one": bf(np.random.standard_normal((N, D_ONE))),
            "h_two_same": bf(np.random.standard_normal((N * NSPIN, D_TWO)) * 2.0 * s[:D_TWO]),
            "h_two_diff": bf(np.random.standard_normal((N * NSPIN, D_TWO)) * 2.0 * s[D_TWO:]),
            "W1": bf(w1),
            "b1": bf(np.random.standard_normal(D_ONE) * 0.3),
            "Wg": bf(np.random.standard_normal((K2, D_ONE)) * 2.0 / np.sqrt(K2))}


def reference(h_one, h_two_same, h_two_diff, W1, b1, Wg):
    h = f64(h_one)
    sqrt2 = np.sqrt(2.0)
    g_mean = h.reshape(G, 2, NSPIN, D_ONE).mean(axis=2)
    g_inp = np.stack([
        np.concatenate([g_mean[:, 0], g_mean[:, 1]], axis=-1),
        np.concatenate([g_mean[:, 1], g_mean[:, 0]], axis=-1),
    ], axis=1).reshape(2 * G, K2)
    pair_same = f64(h_two_same).reshape(N, NSPIN, D_TWO).mean(axis=1)
    pair_diff = f64(h_two_diff).reshape(N, NSPIN, D_TWO).mean(axis=1)
    one_in = np.concatenate([h, pair_same, pair_diff], axis=-1)
    h_new = (mxq(one_in, 1, "e4m3") @ mxq(f64(W1), 0, "e4m3")) + f64(b1)
    global_new = mxq(g_inp, 1, "e4m3") @ mxq(f64(Wg), 0, "e4m3")
    global_new = np.repeat(global_new, NSPIN, axis=0)
    h_new = TANH_GAIN * np.tanh((h_new + global_new) / sqrt2)
    return (h + h_new) / sqrt2

@@ -1,0 +1,178 @@
+import math
+from contextlib import ExitStack
+
+import concourse.mybir as mybir
+from concourse.masks import make_identity
+
+BF16 = mybir.dt.bfloat16
+F32 = mybir.dt.float32
+U32 = mybir.dt.uint32
+U8 = mybir.dt.uint8
+FP8X4 = mybir.dt.float8_e4m3fn_x4
+ADD = mybir.AluOpType.add
+MULT = mybir.AluOpType.mult
+ACT = mybir.ActivationFunctionType
+
+P = 128
+NSPIN = 4
+D_ONE = 256
+D_TWO = 128
+K = 512
+PACK = 4
+TANH_GAIN = 1.5927812698663606
+INV_SQRT2 = 1.0 / math.sqrt(2.0)
+
+FLOPS = 2 * (P * NSPIN) * K * D_ONE + 2 * P * K * D_ONE
+
+
+def quantise_weight(nc, work, raw, codes, scales):
+    grouped = work.tile([P, D_ONE, PACK], BF16, align_bytes=64, tag="w_grouped")
+    nc.scalar.copy(
+        out=grouped[:].rearrange("p (c i) t -> p c t i", i=4),
+        in_=raw.rearrange("p t (c i) -> p c t i", i=4),
+    )
+    nc.vector.quantize_mx(
+        out=codes.bitcast(FP8X4),
+        scales=scales,
+        in_=grouped[:].rearrange("p n t -> p (n t)"),
+    )
+
+
+def tile_fermilayer_pa_s_kernel(tc, h_one, h_two_same, h_two_diff, W1, b1, Wg, out):
+    nc = tc.nc
+    with ExitStack() as ctx:
+        keep = ctx.enter_context(tc.tile_pool(name="keep", bufs=1))
+        work = ctx.enter_context(tc.tile_pool(name="work", bufs=2))
+        psum_t = ctx.enter_context(tc.psum_pool(name="psum_t", bufs=2))
+        psum_g = ctx.enter_context(tc.psum_pool(name="psum_g", bufs=1))
+        psum_acc = ctx.enter_context(tc.psum_pool(name="psum_acc", bufs=NSPIN))
+
+
+        pair_rows = keep.tile([P, 2, NSPIN, NSPIN * D_TWO], BF16)
+        rows = keep.tile([P, NSPIN, K], BF16)
+        w1_raw = keep.tile([P, PACK, D_ONE], BF16)
+        wg_raw = keep.tile([P, PACK, D_ONE], BF16)
+        bias_bc = keep.tile([P, D_ONE], BF16)
+        streams = [
+            s.rearrange("(g i r) d -> g i (r d)", i=NSPIN, r=NSPIN) for s in (h_two_same, h_two_diff)
+        ]
+
+        def load_pair_rows(i):
+            for u in range(2):
+                nc.sync.dma_start(out=pair_rows[:, u, i, :], in_=streams[u][:, i, :])
+
+        load_pair_rows(0)
+        nc.sync.dma_start(out=rows[:, :, 0:D_ONE], in_=h_one.rearrange("(g i) k -> g i k", i=NSPIN))
+        nc.sync.dma_start(out=w1_raw[:], in_=W1.rearrange("(p t) n -> p t n", t=PACK))
+        load_pair_rows(1)
+        nc.sync.dma_start(
+            out=wg_raw[:].rearrange("p (o e) n -> p o (e n)", o=2),
+            in_=Wg.rearrange("(o p e) n -> p o (e n)", o=2, e=2),
+        )
+        load_pair_rows(2)
+        load_pair_rows(3)
+        nc.gpsimd.dma_start(out=bias_bc[:], in_=b1.partition_broadcast(P))
+
+        warm = keep.tile([P, 1], F32)
+        nc.vector.memset(warm[:], 0.0)
+        nc.scalar.activation(out=warm[:], in_=warm[:], func=ACT.Tanh)
+        ident = keep.tile([P, P], F32)
+        make_identity(nc, ident[:])
+        swap = keep.tile([P, P], F32)
+        ident_ms = ident[:].rearrange("p (m s) -> p m s", s=2)
+        swap_ms = swap[:].rearrange("p (m s) -> p m s", s=2)
+        nc.gpsimd.tensor_copy(out=swap_ms[:, :, 0], in_=ident_ms[:, :, 1])
+        nc.gpsimd.tensor_copy(out=swap_ms[:, :, 1], in_=ident_ms[:, :, 0])
+        mean_scale = keep.tile([P, 1], F32)
+        nc.vector.memset(mean_scale[0 : P // 2], 1.0)
+        nc.vector.memset(mean_scale[P // 2 : P], 1.0 / NSPIN)
+
+        h_res = keep.tile([P, NSPIN, D_ONE], F32)
+        nc.scalar.activation(out=h_res[:], in_=rows[:, :, 0:D_ONE], func=ACT.Copy, scale=INV_SQRT2)
+
+        w1_codes = keep.tile([P, D_ONE], U32, align_bytes=64)
+        w1_scales = keep.tile([P, D_ONE], U8, align_bytes=64)
+        wg_codes = keep.tile([P, D_ONE], U32, align_bytes=64)
+        wg_scales = keep.tile([P, D_ONE], U8, align_bytes=64)
+        quantise_weight(nc, work, w1_raw[:], w1_codes[:], w1_scales[:])
+        quantise_weight(nc, work, wg_raw[:], wg_codes[:], wg_scales[:])
+
+        g_half = work.tile([P, 2, D_ONE], F32)
+        nc.vector.tensor_tensor(out=g_half[:], in0=rows[:, 0:2, 0:D_ONE], in1=rows[:, 2:4, 0:D_ONE], op=ADD)
+        g_sum = keep.tile([P, D_ONE], BF16)
+        nc.vector.tensor_tensor(out=g_sum[:], in0=g_half[:, 0, :], in1=g_half[:, 1, :], op=ADD)
+        g_t = psum_g.tile([P, 2, P], F32)
+        nc.tensor.transpose(g_t[:, 0, :], g_sum[:].bitcast(F32), ident[:])
+        nc.tensor.transpose(g_t[:, 1, :], g_sum[:].bitcast(F32), swap[:])
+        g_grouped = keep.tile([P, P, PACK], BF16, align_bytes=64)
+        nc.scalar.activation(
+            out=g_grouped[:].rearrange("p g (o e) -> p g o e", o=2),
+            in_=g_t[:].bitcast(BF16).rearrange("p o (g e) -> p g o e", e=2),
+            func=ACT.Copy,
+            scale=1.0 / NSPIN,
+        )
+        g_codes = keep.tile([P, P], U32, align_bytes=64)
+        g_scales = keep.tile([P, P], U8, align_bytes=64)
+        nc.vector.quantize_mx(
+            out=g_codes[:].bitcast(FP8X4),
+            scales=g_scales[:],
+            in_=g_grouped[:].rearrange("p g t -> p (g t)"),
+        )
+
+        x_codes = keep.tile([P, NSPIN, P], U32, align_bytes=64)
+        x_scales = keep.tile([P, NSPIN, P], U8, align_bytes=64)
+        out_rows = out.rearrange("(g i) f -> g i f", i=NSPIN)
+        for i in range(NSPIN):
+            four = pair_rows[:, :, i, :].rearrange("p u (a b d) -> p u a b d", a=2, b=2)
+            pair_half = work.tile([P, 2, 2, D_TWO], F32)
+            nc.vector.tensor_tensor(out=pair_half[:], in0=four[:, :, :, 0, :], in1=four[:, :, :, 1, :], op=ADD)
+            nc.vector.tensor_tensor(
+                out=rows[:, i, D_ONE:K].rearrange("p (u d) -> p u d", u=2),
+                in0=pair_half[:, :, 0, :],
+                in1=pair_half[:, :, 1, :],
+                op=ADD,
+            )
+            words = rows[:, i, :].bitcast(F32).rearrange("g (p u) -> g p u", u=2)
+            x_t = psum_t.tile([P, 2, P], F32)
+            for u in range(2):
+                nc.tensor.transpose(x_t[:, u, :], words[:, :, u], ident[:])
+            x_grouped = work.tile([P, P, PACK], BF16, align_bytes=64)
+            nc.scalar.activation(
+                out=x_grouped[:].rearrange("p g (u e) -> p g u e", u=2),
+                in_=x_t[:].bitcast(BF16).rearrange("p u (g e) -> p g u e", e=2),
+                func=ACT.Copy,
+                scale=mean_scale[:, 0:1],
+            )
+            nc.vector.quantize_mx(
+                out=x_codes[:, i, :].bitcast(FP8X4),
+                scales=x_scales[:, i, :],
+                in_=x_grouped[:].rearrange("p g t -> p (g t)"),
+            )
+            acc = psum_acc.tile([P, D_ONE], F32)
+            nc.tensor.matmul_mx(
+                out=acc[:],
+                lhsT=x_codes[:, i, :].bitcast(FP8X4),
+                lhsT_scale=x_scales[:, i, :],
+                rhs=w1_codes[:].bitcast(FP8X4),
+                rhs_scale=w1_scales[:],
+                start=True,
+                stop=False,
+            )
+            nc.tensor.matmul_mx(
+                out=acc[:],
+                lhsT=g_codes[:].bitcast(FP8X4),
+                lhsT_scale=g_scales[:],
+                rhs=wg_codes[:].bitcast(FP8X4),
+                rhs_scale=wg_scales[:],
+                start=False,
+                stop=True,
+            )
+            pre = work.tile([P, D_ONE], F32)
+            nc.vector.tensor_tensor(out=pre[:], in0=acc[:], in1=bias_bc[:], op=ADD)
+            th = work.tile([P, D_ONE], F32)
+            nc.scalar.activation(out=th[:], in_=pre[:], func=ACT.Tanh, scale=INV_SQRT2)
+            res = work.tile([P, D_ONE], F32)
+            nc.vector.scalar_tensor_tensor(
+                out=res[:], in0=th[:], scalar=TANH_GAIN * INV_SQRT2, in1=h_res[:, i, :], op0=MULT, op1=ADD
+            )
+            nc.sync.dma_start(out=out_rows[:, i, :], in_=res[:])

@@ -21,21 +21,9 @@ K = 512
 PACK = 4
 TANH_GAIN = 1.5927812698663606
 INV_SQRT2 = 1.0 / math.sqrt(2.0)
+LAG = 2
 
 FLOPS = 2 * (P * NSPIN) * K * D_ONE + 2 * P * K * D_ONE
-
-
-def quantise_weight(nc, work, raw, codes, scales):
-    grouped = work.tile([P, D_ONE, PACK], BF16, align_bytes=64, tag="w_grouped")
-    nc.scalar.copy(
-        out=grouped[:].rearrange("p (c i) t -> p c t i", i=4),
-        in_=raw.rearrange("p t (c i) -> p c t i", i=4),
-    )
-    nc.vector.quantize_mx(
-        out=codes.bitcast(FP8X4),
-        scales=scales,
-        in_=grouped[:].rearrange("p n t -> p (n t)"),
-    )
 
 
 def tile_fermilayer_pa_s_kernel(tc, h_one, h_two_same, h_two_diff, W1, b1, Wg, out):
@@ -43,9 +31,10 @@ def tile_fermilayer_pa_s_kernel(tc, h_one, h_two_same, h_two_diff, W1, b1, Wg, o
     with ExitStack() as ctx:
         keep = ctx.enter_context(tc.tile_pool(name="keep", bufs=1))
         work = ctx.enter_context(tc.tile_pool(name="work", bufs=2))
-        psum_t = ctx.enter_context(tc.psum_pool(name="psum_t", bufs=2))
+        psum_t = ctx.enter_context(tc.psum_pool(name="psum_t", bufs=3))
         psum_g = ctx.enter_context(tc.psum_pool(name="psum_g", bufs=1))
         psum_acc = ctx.enter_context(tc.psum_pool(name="psum_acc", bufs=NSPIN))
+        ctx.enter_context(tc.manual_schedule())
 
 
         pair_rows = keep.tile([P, 2, NSPIN, NSPIN * D_TWO], BF16)
@@ -61,6 +50,7 @@ def tile_fermilayer_pa_s_kernel(tc, h_one, h_two_same, h_two_diff, W1, b1, Wg, o
             for u in range(2):
                 nc.sync.dma_start(out=pair_rows[:, u, i, :], in_=streams[u][:, i, :])
 
+        nc.scalar.dma_start(out=bias_bc[:], in_=b1.partition_broadcast(P))
         load_pair_rows(0)
         nc.sync.dma_start(out=rows[:, :, 0:D_ONE], in_=h_one.rearrange("(g i) k -> g i k", i=NSPIN))
         nc.sync.dma_start(out=w1_raw[:], in_=W1.rearrange("(p t) n -> p t n", t=PACK))
@@ -71,7 +61,6 @@ def tile_fermilayer_pa_s_kernel(tc, h_one, h_two_same, h_two_diff, W1, b1, Wg, o
         )
         load_pair_rows(2)
         load_pair_rows(3)
-        nc.gpsimd.dma_start(out=bias_bc[:], in_=b1.partition_broadcast(P))
 
         warm = keep.tile([P, 1], F32)
         nc.vector.memset(warm[:], 0.0)
@@ -83,76 +72,79 @@ def tile_fermilayer_pa_s_kernel(tc, h_one, h_two_same, h_two_diff, W1, b1, Wg, o
         swap_ms = swap[:].rearrange("p (m s) -> p m s", s=2)
         nc.gpsimd.tensor_copy(out=swap_ms[:, :, 0], in_=ident_ms[:, :, 1])
         nc.gpsimd.tensor_copy(out=swap_ms[:, :, 1], in_=ident_ms[:, :, 0])
-        mean_scale = keep.tile([P, 1], F32)
-        nc.vector.memset(mean_scale[0 : P // 2], 1.0)
-        nc.vector.memset(mean_scale[P // 2 : P], 1.0 / NSPIN)
 
-        h_res = keep.tile([P, NSPIN, D_ONE], F32)
-        nc.scalar.activation(out=h_res[:], in_=rows[:, :, 0:D_ONE], func=ACT.Copy, scale=INV_SQRT2)
-
-        w1_codes = keep.tile([P, D_ONE], U32, align_bytes=64)
-        w1_scales = keep.tile([P, D_ONE], U8, align_bytes=64)
-        wg_codes = keep.tile([P, D_ONE], U32, align_bytes=64)
-        wg_scales = keep.tile([P, D_ONE], U8, align_bytes=64)
-        quantise_weight(nc, work, w1_raw[:], w1_codes[:], w1_scales[:])
-        quantise_weight(nc, work, wg_raw[:], wg_codes[:], wg_scales[:])
-
-        g_half = work.tile([P, 2, D_ONE], F32)
-        nc.vector.tensor_tensor(out=g_half[:], in0=rows[:, 0:2, 0:D_ONE], in1=rows[:, 2:4, 0:D_ONE], op=ADD)
-        g_sum = keep.tile([P, D_ONE], BF16)
-        nc.vector.tensor_tensor(out=g_sum[:], in0=g_half[:, 0, :], in1=g_half[:, 1, :], op=ADD)
-        g_t = psum_g.tile([P, 2, P], F32)
-        nc.tensor.transpose(g_t[:, 0, :], g_sum[:].bitcast(F32), ident[:])
-        nc.tensor.transpose(g_t[:, 1, :], g_sum[:].bitcast(F32), swap[:])
+        x_grouped = keep.tile([P, NSPIN, P, PACK], BF16, align_bytes=64)
         g_grouped = keep.tile([P, P, PACK], BF16, align_bytes=64)
-        nc.scalar.activation(
-            out=g_grouped[:].rearrange("p g (o e) -> p g o e", o=2),
-            in_=g_t[:].bitcast(BF16).rearrange("p o (g e) -> p g o e", e=2),
-            func=ACT.Copy,
-            scale=1.0 / NSPIN,
-        )
-        g_codes = keep.tile([P, P], U32, align_bytes=64)
-        g_scales = keep.tile([P, P], U8, align_bytes=64)
-        nc.vector.quantize_mx(
-            out=g_codes[:].bitcast(FP8X4),
-            scales=g_scales[:],
-            in_=g_grouped[:].rearrange("p g t -> p (g t)"),
-        )
+        w1_grouped = keep.tile([P, D_ONE, PACK], BF16, align_bytes=64)
+        wg_grouped = keep.tile([P, D_ONE, PACK], BF16, align_bytes=64)
 
-        x_codes = keep.tile([P, NSPIN, P], U32, align_bytes=64)
-        x_scales = keep.tile([P, NSPIN, P], U8, align_bytes=64)
-        out_rows = out.rearrange("(g i) f -> g i f", i=NSPIN)
-        for i in range(NSPIN):
+        def electron_tile_operand(i):
             four = pair_rows[:, :, i, :].rearrange("p u (a b d) -> p u a b d", a=2, b=2)
             pair_half = work.tile([P, 2, 2, D_TWO], F32)
             nc.vector.tensor_tensor(out=pair_half[:], in0=four[:, :, :, 0, :], in1=four[:, :, :, 1, :], op=ADD)
-            nc.vector.tensor_tensor(
-                out=rows[:, i, D_ONE:K].rearrange("p (u d) -> p u d", u=2),
-                in0=pair_half[:, :, 0, :],
-                in1=pair_half[:, :, 1, :],
-                op=ADD,
+            pair_sum = work.tile([P, 2, D_TWO], F32)
+            nc.vector.tensor_tensor(out=pair_sum[:], in0=pair_half[:, :, 0, :], in1=pair_half[:, :, 1, :], op=ADD)
+            nc.vector.tensor_scalar_mul(
+                out=rows[:, i, D_ONE:K], in0=pair_sum[:].rearrange("p u d -> p (u d)"), scalar1=1.0 / NSPIN
             )
             words = rows[:, i, :].bitcast(F32).rearrange("g (p u) -> g p u", u=2)
             x_t = psum_t.tile([P, 2, P], F32)
             for u in range(2):
                 nc.tensor.transpose(x_t[:, u, :], words[:, :, u], ident[:])
-            x_grouped = work.tile([P, P, PACK], BF16, align_bytes=64)
-            nc.scalar.activation(
-                out=x_grouped[:].rearrange("p g (u e) -> p g u e", u=2),
-                in_=x_t[:].bitcast(BF16).rearrange("p u (g e) -> p g u e", e=2),
-                func=ACT.Copy,
-                scale=mean_scale[:, 0:1],
+            nc.scalar.copy(
+                out=x_grouped[:, i, :, :].rearrange("p g t -> p (g t)").bitcast(F32).rearrange("p (g u) -> p g u", u=2),
+                in_=x_t[:].rearrange("p u g -> p g u"),
             )
-            nc.vector.quantize_mx(
-                out=x_codes[:, i, :].bitcast(FP8X4),
-                scales=x_scales[:, i, :],
-                in_=x_grouped[:].rearrange("p g t -> p (g t)"),
+
+        def group_operand():
+            g_t = psum_g.tile([P, 2, P], F32)
+            nc.tensor.transpose(g_t[:, 0, :], g_mean[:].bitcast(F32), ident[:])
+            nc.tensor.transpose(g_t[:, 1, :], g_mean[:].bitcast(F32), swap[:])
+            nc.scalar.copy(
+                out=g_grouped[:].rearrange("p g t -> p (g t)").bitcast(F32).rearrange("p (g o) -> p g o", o=2),
+                in_=g_t[:].rearrange("p o g -> p g o"),
             )
+
+        def regroup_weight(copy, grouped, raw):
+            copy(
+                out=grouped[:].rearrange("p (c i) t -> p c t i", i=4),
+                in_=raw[:].rearrange("p t (c i) -> p c t i", i=4),
+            )
+
+        h_res = keep.tile([P, NSPIN, D_ONE], F32)
+        nc.scalar.activation(out=h_res[:], in_=rows[:, :, 0:D_ONE], func=ACT.Copy, scale=INV_SQRT2)
+        g_half = keep.tile([P, 2, D_ONE], F32)
+        g_sum = keep.tile([P, D_ONE], F32)
+        g_mean = keep.tile([P, D_ONE], BF16)
+        nc.gpsimd.tensor_tensor(out=g_half[:], in0=rows[:, 0:2, 0:D_ONE], in1=rows[:, 2:4, 0:D_ONE], op=ADD)
+        nc.gpsimd.tensor_tensor(out=g_sum[:], in0=g_half[:, 0, :], in1=g_half[:, 1, :], op=ADD)
+        nc.gpsimd.tensor_scalar(out=g_mean[:], in0=g_sum[:], scalar1=1.0 / NSPIN, scalar2=0.0, op0=MULT, op1=ADD)
+
+        electron_tile_operand(0)
+        regroup_weight(nc.vector.tensor_copy, w1_grouped, w1_raw)
+        regroup_weight(nc.scalar.copy, wg_grouped, wg_raw)
+        group_operand()
+        electron_tile_operand(1)
+        electron_tile_operand(2)
+        electron_tile_operand(3)
+
+        def quantise(name, grouped, width):
+            codes = keep.tile([P, width], U32, align_bytes=64, name=name + "_codes")
+            scales = keep.tile([P, width], U8, align_bytes=64, name=name + "_scales")
+            nc.vector.quantize_mx(out=codes[:].bitcast(FP8X4), scales=scales[:], in_=grouped)
+            return codes, scales
+
+        w1_codes, w1_scales = quantise("w1", w1_grouped[:].rearrange("p n t -> p (n t)"), D_ONE)
+        g_codes, g_scales = quantise("g", g_grouped[:].rearrange("p g t -> p (g t)"), P)
+        wg_codes, wg_scales = quantise("wg", wg_grouped[:].rearrange("p n t -> p (n t)"), D_ONE)
+        accs = []
+        for i in range(NSPIN):
+            x_codes, x_scales = quantise("x%d" % i, x_grouped[:, i, :, :].rearrange("p g t -> p (g t)"), P)
             acc = psum_acc.tile([P, D_ONE], F32)
             nc.tensor.matmul_mx(
                 out=acc[:],
-                lhsT=x_codes[:, i, :].bitcast(FP8X4),
-                lhsT_scale=x_scales[:, i, :],
+                lhsT=x_codes[:].bitcast(FP8X4),
+                lhsT_scale=x_scales[:],
                 rhs=w1_codes[:].bitcast(FP8X4),
                 rhs_scale=w1_scales[:],
                 start=True,
@@ -167,12 +159,22 @@ def tile_fermilayer_pa_s_kernel(tc, h_one, h_two_same, h_two_diff, W1, b1, Wg, o
                 start=False,
                 stop=True,
             )
-            pre = work.tile([P, D_ONE], F32)
-            nc.vector.tensor_tensor(out=pre[:], in0=acc[:], in1=bias_bc[:], op=ADD)
-            th = work.tile([P, D_ONE], F32)
-            nc.scalar.activation(out=th[:], in_=pre[:], func=ACT.Tanh, scale=INV_SQRT2)
-            res = work.tile([P, D_ONE], F32)
+            accs.append(acc)
+
+        out_rows = out.rearrange("(g i) f -> g i f", i=NSPIN)
+        th = keep.tile([P, NSPIN, D_ONE], F32)
+        res = keep.tile([P, NSPIN, D_ONE], F32)
+
+        def finish(i):
             nc.vector.scalar_tensor_tensor(
-                out=res[:], in0=th[:], scalar=TANH_GAIN * INV_SQRT2, in1=h_res[:, i, :], op0=MULT, op1=ADD
+                out=res[:, i, :], in0=th[:, i, :], scalar=TANH_GAIN * INV_SQRT2, in1=h_res[:, i, :], op0=MULT, op1=ADD
             )
-            nc.sync.dma_start(out=out_rows[:, i, :], in_=res[:])
+            nc.sync.dma_start(out=out_rows[:, i, :], in_=res[:, i, :])
+
+        pre = keep.tile([P, NSPIN, D_ONE], F32)
+        for i in range(NSPIN + LAG):
+            if i < NSPIN:
+                nc.vector.tensor_tensor(out=pre[:, i, :], in0=accs[i][:], in1=bias_bc[:], op=ADD)
+                nc.scalar.activation(out=th[:, i, :], in_=pre[:, i, :], func=ACT.Tanh, scale=INV_SQRT2)
+            if i >= LAG:
+                finish(i - LAG)

@@ -31,7 +31,7 @@ def tile_fermilayer_pa_s_kernel(tc, h_one, h_two_same, h_two_diff, W1, b1, Wg, o
     with ExitStack() as ctx:
         keep = ctx.enter_context(tc.tile_pool(name="keep", bufs=1))
         work = ctx.enter_context(tc.tile_pool(name="work", bufs=2))
-        psum_t = ctx.enter_context(tc.psum_pool(name="psum_t", bufs=3))
+        psum_t = ctx.enter_context(tc.psum_pool(name="psum_t", bufs=2))
         psum_g = ctx.enter_context(tc.psum_pool(name="psum_g", bufs=1))
         psum_acc = ctx.enter_context(tc.psum_pool(name="psum_acc", bufs=NSPIN))
         ctx.enter_context(tc.manual_schedule())
@@ -41,7 +41,6 @@ def tile_fermilayer_pa_s_kernel(tc, h_one, h_two_same, h_two_diff, W1, b1, Wg, o
         rows = keep.tile([P, NSPIN, K], BF16)
         w1_raw = keep.tile([P, PACK, D_ONE], BF16)
         wg_raw = keep.tile([P, PACK, D_ONE], BF16)
-        bias_bc = keep.tile([P, D_ONE], BF16)
         streams = [
             s.rearrange("(g i r) d -> g i (r d)", i=NSPIN, r=NSPIN) for s in (h_two_same, h_two_diff)
         ]
@@ -50,21 +49,30 @@ def tile_fermilayer_pa_s_kernel(tc, h_one, h_two_same, h_two_diff, W1, b1, Wg, o
             for u in range(2):
                 nc.sync.dma_start(out=pair_rows[:, u, i, :], in_=streams[u][:, i, :])
 
-        nc.scalar.dma_start(out=bias_bc[:], in_=b1.partition_broadcast(P))
         load_pair_rows(0)
-        nc.sync.dma_start(out=rows[:, :, 0:D_ONE], in_=h_one.rearrange("(g i) k -> g i k", i=NSPIN))
-        nc.sync.dma_start(out=w1_raw[:], in_=W1.rearrange("(p t) n -> p t n", t=PACK))
         load_pair_rows(1)
+        nc.sync.dma_start(out=rows[:, :, 0:D_ONE], in_=h_one.rearrange("(g i) k -> g i k", i=NSPIN))
+        load_pair_rows(2)
+        load_pair_rows(3)
+        nc.sync.dma_start(out=w1_raw[:], in_=W1.rearrange("(p t) n -> p t n", t=PACK))
         nc.sync.dma_start(
             out=wg_raw[:].rearrange("p (o e) n -> p o (e n)", o=2),
             in_=Wg.rearrange("(o p e) n -> p o (e n)", o=2, e=2),
         )
-        load_pair_rows(2)
-        load_pair_rows(3)
+
+        ones = keep.tile([P, P], BF16)
+        nc.vector.memset(ones[:], 1.0)
+        bias_row = keep.tile([P, D_ONE], BF16)
+        nc.vector.memset(bias_row[:], 0.0)
+        nc.scalar.dma_start(out=bias_row[0:1, :], in_=b1.rearrange("(o n) -> o n", o=1))
+        bias_ps = psum_g.tile([P, D_ONE], F32)
+        nc.tensor.matmul(out=bias_ps[:], lhsT=ones[:], rhs=bias_row[:], start=True, stop=True)
+        bias_bc = keep.tile([P, D_ONE], F32)
 
         warm = keep.tile([P, 1], F32)
         nc.vector.memset(warm[:], 0.0)
         nc.scalar.activation(out=warm[:], in_=warm[:], func=ACT.Tanh)
+        nc.scalar.copy(out=bias_bc[:], in_=bias_ps[:])
         ident = keep.tile([P, P], F32)
         make_identity(nc, ident[:])
         swap = keep.tile([P, P], F32)
@@ -72,37 +80,53 @@ def tile_fermilayer_pa_s_kernel(tc, h_one, h_two_same, h_two_diff, W1, b1, Wg, o
         swap_ms = swap[:].rearrange("p (m s) -> p m s", s=2)
         nc.gpsimd.tensor_copy(out=swap_ms[:, :, 0], in_=ident_ms[:, :, 1])
         nc.gpsimd.tensor_copy(out=swap_ms[:, :, 1], in_=ident_ms[:, :, 0])
+        mean_scale = keep.tile([P, 1], F32)
+        nc.vector.memset(mean_scale[0 : P // 2], 1.0)
+        nc.vector.memset(mean_scale[P // 2 : P], 1.0 / NSPIN)
 
         x_grouped = keep.tile([P, NSPIN, P, PACK], BF16, align_bytes=64)
         g_grouped = keep.tile([P, P, PACK], BF16, align_bytes=64)
         w1_grouped = keep.tile([P, D_ONE, PACK], BF16, align_bytes=64)
         wg_grouped = keep.tile([P, D_ONE, PACK], BF16, align_bytes=64)
 
-        def electron_tile_operand(i):
+        pair_half = keep.tile([P, NSPIN, 2, 2, D_TWO], F32)
+        g_half = keep.tile([P, 2, D_ONE], F32)
+        g_sum = keep.tile([P, D_ONE], BF16)
+
+        def pair_sums_of_two(i):
             four = pair_rows[:, :, i, :].rearrange("p u (a b d) -> p u a b d", a=2, b=2)
-            pair_half = work.tile([P, 2, 2, D_TWO], F32)
-            nc.vector.tensor_tensor(out=pair_half[:], in0=four[:, :, :, 0, :], in1=four[:, :, :, 1, :], op=ADD)
-            pair_sum = work.tile([P, 2, D_TWO], F32)
-            nc.vector.tensor_tensor(out=pair_sum[:], in0=pair_half[:, :, 0, :], in1=pair_half[:, :, 1, :], op=ADD)
-            nc.vector.tensor_scalar_mul(
-                out=rows[:, i, D_ONE:K], in0=pair_sum[:].rearrange("p u d -> p (u d)"), scalar1=1.0 / NSPIN
+            nc.vector.tensor_tensor(
+                out=pair_half[:, i, :, :, :], in0=four[:, :, :, 0, :], in1=four[:, :, :, 1, :], op=ADD
+            )
+
+        def electron_tile_operand(i):
+            nc.vector.tensor_tensor(
+                out=rows[:, i, D_ONE:K].rearrange("p (u d) -> p u d", u=2),
+                in0=pair_half[:, i, :, 0, :],
+                in1=pair_half[:, i, :, 1, :],
+                op=ADD,
             )
             words = rows[:, i, :].bitcast(F32).rearrange("g (p u) -> g p u", u=2)
             x_t = psum_t.tile([P, 2, P], F32)
             for u in range(2):
                 nc.tensor.transpose(x_t[:, u, :], words[:, :, u], ident[:])
-            nc.scalar.copy(
-                out=x_grouped[:, i, :, :].rearrange("p g t -> p (g t)").bitcast(F32).rearrange("p (g u) -> p g u", u=2),
-                in_=x_t[:].rearrange("p u g -> p g u"),
+            nc.scalar.activation(
+                out=x_grouped[:, i, :, :].rearrange("p g (u e) -> p g u e", u=2),
+                in_=x_t[:].bitcast(BF16).rearrange("p u (g e) -> p g u e", e=2),
+                func=ACT.Copy,
+                scale=mean_scale[:, 0:1],
             )
 
         def group_operand():
+            nc.vector.tensor_tensor(out=g_sum[:], in0=g_half[:, 0, :], in1=g_half[:, 1, :], op=ADD)
             g_t = psum_g.tile([P, 2, P], F32)
-            nc.tensor.transpose(g_t[:, 0, :], g_mean[:].bitcast(F32), ident[:])
-            nc.tensor.transpose(g_t[:, 1, :], g_mean[:].bitcast(F32), swap[:])
-            nc.scalar.copy(
-                out=g_grouped[:].rearrange("p g t -> p (g t)").bitcast(F32).rearrange("p (g o) -> p g o", o=2),
-                in_=g_t[:].rearrange("p o g -> p g o"),
+            nc.tensor.transpose(g_t[:, 0, :], g_sum[:].bitcast(F32), ident[:])
+            nc.tensor.transpose(g_t[:, 1, :], g_sum[:].bitcast(F32), swap[:])
+            nc.scalar.activation(
+                out=g_grouped[:].rearrange("p g (o e) -> p g o e", o=2),
+                in_=g_t[:].bitcast(BF16).rearrange("p o (g e) -> p g o e", e=2),
+                func=ACT.Copy,
+                scale=1.0 / NSPIN,
             )
 
         def regroup_weight(copy, grouped, raw):
@@ -111,22 +135,21 @@ def tile_fermilayer_pa_s_kernel(tc, h_one, h_two_same, h_two_diff, W1, b1, Wg, o
                 in_=raw[:].rearrange("p t (c i) -> p c t i", i=4),
             )
 
+        pair_sums_of_two(0)
+        pair_sums_of_two(1)
+        electron_tile_operand(0)
+        nc.vector.tensor_tensor(out=g_half[:], in0=rows[:, 0:2, 0:D_ONE], in1=rows[:, 2:4, 0:D_ONE], op=ADD)
+        electron_tile_operand(1)
+        pair_sums_of_two(2)
+        group_operand()
+        pair_sums_of_two(3)
+        electron_tile_operand(2)
+        regroup_weight(nc.scalar.copy, w1_grouped, w1_raw)
+        regroup_weight(nc.vector.tensor_copy, wg_grouped, wg_raw)
+        electron_tile_operand(3)
+
         h_res = keep.tile([P, NSPIN, D_ONE], F32)
         nc.scalar.activation(out=h_res[:], in_=rows[:, :, 0:D_ONE], func=ACT.Copy, scale=INV_SQRT2)
-        g_half = keep.tile([P, 2, D_ONE], F32)
-        g_sum = keep.tile([P, D_ONE], F32)
-        g_mean = keep.tile([P, D_ONE], BF16)
-        nc.gpsimd.tensor_tensor(out=g_half[:], in0=rows[:, 0:2, 0:D_ONE], in1=rows[:, 2:4, 0:D_ONE], op=ADD)
-        nc.gpsimd.tensor_tensor(out=g_sum[:], in0=g_half[:, 0, :], in1=g_half[:, 1, :], op=ADD)
-        nc.gpsimd.tensor_scalar(out=g_mean[:], in0=g_sum[:], scalar1=1.0 / NSPIN, scalar2=0.0, op0=MULT, op1=ADD)
-
-        electron_tile_operand(0)
-        regroup_weight(nc.vector.tensor_copy, w1_grouped, w1_raw)
-        regroup_weight(nc.scalar.copy, wg_grouped, wg_raw)
-        group_operand()
-        electron_tile_operand(1)
-        electron_tile_operand(2)
-        electron_tile_operand(3)
 
         def quantise(name, grouped, width):
             codes = keep.tile([P, width], U32, align_bytes=64, name=name + "_codes")
@@ -134,8 +157,8 @@ def tile_fermilayer_pa_s_kernel(tc, h_one, h_two_same, h_two_diff, W1, b1, Wg, o
             nc.vector.quantize_mx(out=codes[:].bitcast(FP8X4), scales=scales[:], in_=grouped)
             return codes, scales
 
-        w1_codes, w1_scales = quantise("w1", w1_grouped[:].rearrange("p n t -> p (n t)"), D_ONE)
         g_codes, g_scales = quantise("g", g_grouped[:].rearrange("p g t -> p (g t)"), P)
+        w1_codes, w1_scales = quantise("w1", w1_grouped[:].rearrange("p n t -> p (n t)"), D_ONE)
         wg_codes, wg_scales = quantise("wg", wg_grouped[:].rearrange("p n t -> p (n t)"), D_ONE)
         accs = []
         for i in range(NSPIN):
@@ -162,19 +185,16 @@ def tile_fermilayer_pa_s_kernel(tc, h_one, h_two_same, h_two_diff, W1, b1, Wg, o
             accs.append(acc)
 
         out_rows = out.rearrange("(g i) f -> g i f", i=NSPIN)
+        pre = keep.tile([P, NSPIN, D_ONE], F32)
         th = keep.tile([P, NSPIN, D_ONE], F32)
         res = keep.tile([P, NSPIN, D_ONE], F32)
-
-        def finish(i):
-            nc.vector.scalar_tensor_tensor(
-                out=res[:, i, :], in0=th[:, i, :], scalar=TANH_GAIN * INV_SQRT2, in1=h_res[:, i, :], op0=MULT, op1=ADD
-            )
-            nc.sync.dma_start(out=out_rows[:, i, :], in_=res[:, i, :])
-
-        pre = keep.tile([P, NSPIN, D_ONE], F32)
         for i in range(NSPIN + LAG):
             if i < NSPIN:
                 nc.vector.tensor_tensor(out=pre[:, i, :], in0=accs[i][:], in1=bias_bc[:], op=ADD)
                 nc.scalar.activation(out=th[:, i, :], in_=pre[:, i, :], func=ACT.Tanh, scale=INV_SQRT2)
             if i >= LAG:
-                finish(i - LAG)
+                j = i - LAG
+                nc.vector.scalar_tensor_tensor(
+                    out=res[:, j, :], in0=th[:, j, :], scalar=TANH_GAIN * INV_SQRT2, in1=h_res[:, j, :], op0=MULT, op1=ADD
+                )
+                nc.sync.dma_start(out=out_rows[:, j, :], in_=res[:, j, :])

@@ -50,11 +50,11 @@ def tile_fermilayer_pa_s_kernel(tc, h_one, h_two_same, h_two_diff, W1, b1, Wg, o
                 nc.sync.dma_start(out=pair_rows[:, u, i, :], in_=streams[u][:, i, :])
 
         load_pair_rows(0)
+        nc.sync.dma_start(out=w1_raw[:], in_=W1.rearrange("(p t) n -> p t n", t=PACK))
         load_pair_rows(1)
         nc.sync.dma_start(out=rows[:, :, 0:D_ONE], in_=h_one.rearrange("(g i) k -> g i k", i=NSPIN))
         load_pair_rows(2)
         load_pair_rows(3)
-        nc.sync.dma_start(out=w1_raw[:], in_=W1.rearrange("(p t) n -> p t n", t=PACK))
         nc.sync.dma_start(
             out=wg_raw[:].rearrange("p (o e) n -> p o (e n)", o=2),
             in_=Wg.rearrange("(o p e) n -> p o (e n)", o=2, e=2),
@@ -135,18 +135,18 @@ def tile_fermilayer_pa_s_kernel(tc, h_one, h_two_same, h_two_diff, W1, b1, Wg, o
                 in_=raw[:].rearrange("p t (c i) -> p c t i", i=4),
             )
 
+        regroup_weight(nc.scalar.copy, w1_grouped, w1_raw)
         pair_sums_of_two(0)
-        pair_sums_of_two(1)
         electron_tile_operand(0)
+        pair_sums_of_two(1)
         nc.vector.tensor_tensor(out=g_half[:], in0=rows[:, 0:2, 0:D_ONE], in1=rows[:, 2:4, 0:D_ONE], op=ADD)
         electron_tile_operand(1)
         pair_sums_of_two(2)
         group_operand()
         pair_sums_of_two(3)
         electron_tile_operand(2)
-        regroup_weight(nc.scalar.copy, w1_grouped, w1_raw)
-        regroup_weight(nc.vector.tensor_copy, wg_grouped, wg_raw)
         electron_tile_operand(3)
+        regroup_weight(nc.vector.tensor_copy, wg_grouped, wg_raw)
 
         h_res = keep.tile([P, NSPIN, D_ONE], F32)
         nc.scalar.activation(out=h_res[:], in_=rows[:, :, 0:D_ONE], func=ACT.Copy, scale=INV_SQRT2)
@@ -157,8 +157,8 @@ def tile_fermilayer_pa_s_kernel(tc, h_one, h_two_same, h_two_diff, W1, b1, Wg, o
             nc.vector.quantize_mx(out=codes[:].bitcast(FP8X4), scales=scales[:], in_=grouped)
             return codes, scales
 
-        g_codes, g_scales = quantise("g", g_grouped[:].rearrange("p g t -> p (g t)"), P)
         w1_codes, w1_scales = quantise("w1", w1_grouped[:].rearrange("p n t -> p (n t)"), D_ONE)
+        g_codes, g_scales = quantise("g", g_grouped[:].rearrange("p g t -> p (g t)"), P)
         wg_codes, wg_scales = quantise("wg", wg_grouped[:].rearrange("p n t -> p (n t)"), D_ONE)
         accs = []
         for i in range(NSPIN):

@@ -21,7 +21,6 @@ K = 512
 PACK = 4
 TANH_GAIN = 1.5927812698663606
 INV_SQRT2 = 1.0 / math.sqrt(2.0)
-LAG = 2
 
 FLOPS = 2 * (P * NSPIN) * K * D_ONE + 2 * P * K * D_ONE
 
@@ -30,171 +29,255 @@ def tile_fermilayer_pa_s_kernel(tc, h_one, h_two_same, h_two_diff, W1, b1, Wg, o
     nc = tc.nc
     with ExitStack() as ctx:
         keep = ctx.enter_context(tc.tile_pool(name="keep", bufs=1))
-        work = ctx.enter_context(tc.tile_pool(name="work", bufs=2))
         psum_t = ctx.enter_context(tc.psum_pool(name="psum_t", bufs=2))
         psum_g = ctx.enter_context(tc.psum_pool(name="psum_g", bufs=1))
         psum_acc = ctx.enter_context(tc.psum_pool(name="psum_acc", bufs=NSPIN))
         ctx.enter_context(tc.manual_schedule())
 
-
         pair_rows = keep.tile([P, 2, NSPIN, NSPIN * D_TWO], BF16)
         rows = keep.tile([P, NSPIN, K], BF16)
+        h_nat = keep.tile([P, NSPIN, D_ONE], BF16)
         w1_raw = keep.tile([P, PACK, D_ONE], BF16)
         wg_raw = keep.tile([P, PACK, D_ONE], BF16)
+        bias_row = keep.tile([P, D_ONE], BF16)
         streams = [
             s.rearrange("(g i r) d -> g i (r d)", i=NSPIN, r=NSPIN) for s in (h_two_same, h_two_diff)
         ]
 
-        def load_pair_rows(i):
-            for u in range(2):
-                nc.sync.dma_start(out=pair_rows[:, u, i, :], in_=streams[u][:, i, :])
+        def load_pair(u, i):
+            nc.sync.dma_start(out=pair_rows[:, u, i, :], in_=streams[u][:, i, :])
 
-        load_pair_rows(0)
-        nc.sync.dma_start(out=w1_raw[:], in_=W1.rearrange("(p t) n -> p t n", t=PACK))
-        load_pair_rows(1)
-        nc.sync.dma_start(out=rows[:, :, 0:D_ONE], in_=h_one.rearrange("(g i) k -> g i k", i=NSPIN))
-        load_pair_rows(2)
-        load_pair_rows(3)
-        nc.sync.dma_start(
-            out=wg_raw[:].rearrange("p (o e) n -> p o (e n)", o=2),
-            in_=Wg.rearrange("(o p e) n -> p o (e n)", o=2, e=2),
-        )
+        def load_h():
+            nc.sync.dma_start(out=rows[:, :, 0:D_ONE], in_=h_one.rearrange("(g i) k -> g i k", i=NSPIN))
 
+        def load_h_nat():
+            nc.sync.dma_start(out=h_nat[:], in_=h_one.rearrange("(r q) k -> q r k", q=P))
+
+        def load_w1():
+            nc.sync.dma_start(out=w1_raw[:], in_=W1.rearrange("(p t) n -> p t n", t=PACK))
+
+        def load_wg():
+            nc.sync.dma_start(
+                out=wg_raw[:].rearrange("p (o e) n -> p o (e n)", o=2),
+                in_=Wg.rearrange("(o p e) n -> p o (e n)", o=2, e=2),
+            )
+
+        nc.vector.memset(bias_row[:], 0.0)
         ones = keep.tile([P, P], BF16)
         nc.vector.memset(ones[:], 1.0)
-        bias_row = keep.tile([P, D_ONE], BF16)
-        nc.vector.memset(bias_row[:], 0.0)
-        nc.scalar.dma_start(out=bias_row[0:1, :], in_=b1.rearrange("(o n) -> o n", o=1))
-        bias_ps = psum_g.tile([P, D_ONE], F32)
-        nc.tensor.matmul(out=bias_ps[:], lhsT=ones[:], rhs=bias_row[:], start=True, stop=True)
-        bias_bc = keep.tile([P, D_ONE], F32)
-
         warm = keep.tile([P, 1], F32)
         nc.vector.memset(warm[:], 0.0)
-        nc.scalar.activation(out=warm[:], in_=warm[:], func=ACT.Tanh)
-        nc.scalar.copy(out=bias_bc[:], in_=bias_ps[:])
-        ident = keep.tile([P, P], F32)
-        make_identity(nc, ident[:])
-        swap = keep.tile([P, P], F32)
-        ident_ms = ident[:].rearrange("p (m s) -> p m s", s=2)
-        swap_ms = swap[:].rearrange("p (m s) -> p m s", s=2)
-        nc.gpsimd.tensor_copy(out=swap_ms[:, :, 0], in_=ident_ms[:, :, 1])
-        nc.gpsimd.tensor_copy(out=swap_ms[:, :, 1], in_=ident_ms[:, :, 0])
         mean_scale = keep.tile([P, 1], F32)
         nc.vector.memset(mean_scale[0 : P // 2], 1.0)
         nc.vector.memset(mean_scale[P // 2 : P], 1.0 / NSPIN)
+        load_pair(0, 0)
+        load_pair(1, 0)
+        load_pair(0, 1)
+        load_pair(1, 1)
+        load_h()
+        load_pair(0, 2)
+        load_pair(1, 2)
+        load_w1()
+        load_pair(0, 3)
+        load_pair(1, 3)
+        load_h_nat()
+        load_wg()
+        nc.sync.dma_start(out=bias_row[0:1, :], in_=b1.rearrange("(o n) -> o n", o=1))
+        nc.scalar.activation(out=warm[:], in_=warm[:], func=ACT.Tanh)
+        ident = keep.tile([P, P], F32)
+        make_identity(nc, ident[:])
+        sum_groups = keep.tile([P, P // NSPIN], BF16)
+        with nc.allow_low_precision(reason="sums of one 1 and zeros"):
+            nc.vector.tensor_reduce(
+                out=sum_groups[:], in_=ident[:].rearrange("q (g i) -> q g i", i=NSPIN), axis=mybir.AxisListType.X, op=ADD
+            )
 
         x_grouped = keep.tile([P, NSPIN, P, PACK], BF16, align_bytes=64)
         g_grouped = keep.tile([P, P, PACK], BF16, align_bytes=64)
         w1_grouped = keep.tile([P, D_ONE, PACK], BF16, align_bytes=64)
         wg_grouped = keep.tile([P, D_ONE, PACK], BF16, align_bytes=64)
-
         pair_half = keep.tile([P, NSPIN, 2, 2, D_TWO], F32)
-        g_half = keep.tile([P, 2, D_ONE], F32)
-        g_sum = keep.tile([P, D_ONE], BF16)
+        bias_bc = keep.tile([P, D_ONE], F32)
+        h_res = keep.tile([P, NSPIN, D_ONE], F32)
+        pre = keep.tile([P, NSPIN, D_ONE], F32)
+        th = keep.tile([P, NSPIN, D_ONE], F32)
+        res = keep.tile([P, NSPIN, D_ONE], F32)
+        out_rows = out.rearrange("(g i) f -> g i f", i=NSPIN)
+        x_ts, accs, operands = {}, {}, {}
 
-        def pair_sums_of_two(i):
+        def s1(i):
             four = pair_rows[:, :, i, :].rearrange("p u (a b d) -> p u a b d", a=2, b=2)
             nc.vector.tensor_tensor(
                 out=pair_half[:, i, :, :, :], in0=four[:, :, :, 0, :], in1=four[:, :, :, 1, :], op=ADD
             )
 
-        def electron_tile_operand(i):
+        def s2(i):
             nc.vector.tensor_tensor(
                 out=rows[:, i, D_ONE:K].rearrange("p (u d) -> p u d", u=2),
                 in0=pair_half[:, i, :, 0, :],
                 in1=pair_half[:, i, :, 1, :],
                 op=ADD,
             )
+
+        def xt(i):
             words = rows[:, i, :].bitcast(F32).rearrange("g (p u) -> g p u", u=2)
             x_t = psum_t.tile([P, 2, P], F32)
             for u in range(2):
                 nc.tensor.transpose(x_t[:, u, :], words[:, :, u], ident[:])
-            nc.scalar.activation(
-                out=x_grouped[:, i, :, :].rearrange("p g (u e) -> p g u e", u=2),
-                in_=x_t[:].bitcast(BF16).rearrange("p u (g e) -> p g u e", e=2),
-                func=ACT.Copy,
-                scale=mean_scale[:, 0:1],
+            x_ts[i] = x_t
+
+        def xc(i, copy=nc.scalar.copy):
+            copy(
+                out=x_grouped[:, i, :, :].rearrange("p g t -> p (g t)").bitcast(F32).rearrange("p (g u) -> p g u", u=2),
+                in_=x_ts[i][:].rearrange("p u g -> p g u"),
             )
 
-        def group_operand():
-            nc.vector.tensor_tensor(out=g_sum[:], in0=g_half[:, 0, :], in1=g_half[:, 1, :], op=ADD)
+        def g_sums():
             g_t = psum_g.tile([P, 2, P], F32)
-            nc.tensor.transpose(g_t[:, 0, :], g_sum[:].bitcast(F32), ident[:])
-            nc.tensor.transpose(g_t[:, 1, :], g_sum[:].bitcast(F32), swap[:])
+            x_ts["g"] = g_t
+            for e in range(2):
+                for r in range(NSPIN):
+                    cols = slice(r * P // NSPIN, (r + 1) * P // NSPIN)
+                    nc.tensor.matmul(
+                        out=g_t[:, e, cols],
+                        lhsT=h_nat[:, r, :].rearrange("q (c e) -> q c e", e=2)[:, :, e],
+                        rhs=sum_groups[:],
+                        start=True,
+                        stop=True,
+                    )
+
+        def g_copy_own():
             nc.scalar.activation(
-                out=g_grouped[:].rearrange("p g (o e) -> p g o e", o=2),
-                in_=g_t[:].bitcast(BF16).rearrange("p o (g e) -> p g o e", e=2),
+                out=g_grouped[:, :, 0:2], in_=x_ts["g"][:].rearrange("p e g -> p g e"), func=ACT.Copy, scale=1.0 / NSPIN
+            )
+
+        def g_copy_other():
+            nc.scalar.activation(
+                out=g_grouped[:, :, 2:4].rearrange("p (m s) e -> p m s e", s=2),
+                in_=x_ts["g"][:].rearrange("p e (m s) -> p m s e", s=2)[:, :, ::-1, :],
                 func=ACT.Copy,
                 scale=1.0 / NSPIN,
             )
 
-        def regroup_weight(copy, grouped, raw):
-            copy(
-                out=grouped[:].rearrange("p (c i) t -> p c t i", i=4),
-                in_=raw[:].rearrange("p t (c i) -> p c t i", i=4),
+        def bias():
+            bias_ps = psum_g.tile([P, D_ONE], F32)
+            nc.tensor.matmul(out=bias_ps[:], lhsT=ones[:], rhs=bias_row[:], start=True, stop=True)
+            nc.scalar.copy(out=bias_bc[:], in_=bias_ps[:])
+
+        def w1_regroup():
+            nc.scalar.activation(
+                out=w1_grouped[:].rearrange("p (c i) t -> p c t i", i=4),
+                in_=w1_raw[:].rearrange("p t (c i) -> p c t i", i=4),
+                func=ACT.Copy,
+                scale=mean_scale[:, 0:1],
             )
 
-        regroup_weight(nc.scalar.copy, w1_grouped, w1_raw)
-        pair_sums_of_two(0)
-        electron_tile_operand(0)
-        pair_sums_of_two(1)
-        nc.vector.tensor_tensor(out=g_half[:], in0=rows[:, 0:2, 0:D_ONE], in1=rows[:, 2:4, 0:D_ONE], op=ADD)
-        electron_tile_operand(1)
-        pair_sums_of_two(2)
-        group_operand()
-        pair_sums_of_two(3)
-        electron_tile_operand(2)
-        electron_tile_operand(3)
-        regroup_weight(nc.vector.tensor_copy, wg_grouped, wg_raw)
+        def wg_regroup(copy):
+            copy(
+                out=wg_grouped[:].rearrange("p (c i) t -> p c t i", i=4),
+                in_=wg_raw[:].rearrange("p t (c i) -> p c t i", i=4),
+            )
 
-        h_res = keep.tile([P, NSPIN, D_ONE], F32)
-        nc.scalar.activation(out=h_res[:], in_=rows[:, :, 0:D_ONE], func=ACT.Copy, scale=INV_SQRT2)
+        def residual_term():
+            nc.scalar.activation(out=h_res[:], in_=rows[:, :, 0:D_ONE], func=ACT.Copy, scale=INV_SQRT2)
 
         def quantise(name, grouped, width):
             codes = keep.tile([P, width], U32, align_bytes=64, name=name + "_codes")
             scales = keep.tile([P, width], U8, align_bytes=64, name=name + "_scales")
             nc.vector.quantize_mx(out=codes[:].bitcast(FP8X4), scales=scales[:], in_=grouped)
-            return codes, scales
+            operands[name] = codes, scales
 
-        w1_codes, w1_scales = quantise("w1", w1_grouped[:].rearrange("p n t -> p (n t)"), D_ONE)
-        g_codes, g_scales = quantise("g", g_grouped[:].rearrange("p g t -> p (g t)"), P)
-        wg_codes, wg_scales = quantise("wg", wg_grouped[:].rearrange("p n t -> p (n t)"), D_ONE)
-        accs = []
-        for i in range(NSPIN):
-            x_codes, x_scales = quantise("x%d" % i, x_grouped[:, i, :, :].rearrange("p g t -> p (g t)"), P)
+        def q_w1():
+            quantise("w1", w1_grouped[:].rearrange("p n t -> p (n t)"), D_ONE)
+
+        def q_wg():
+            quantise("wg", wg_grouped[:].rearrange("p n t -> p (n t)"), D_ONE)
+
+        def q_g():
+            quantise("g", g_grouped[:].rearrange("p g t -> p (g t)"), P)
+
+        def q_x(i):
+            quantise("x%d" % i, x_grouped[:, i, :, :].rearrange("p g t -> p (g t)"), P)
+
+        def mx(acc, left, right, start):
+            nc.tensor.matmul_mx(
+                out=acc[:],
+                lhsT=operands[left][0][:].bitcast(FP8X4),
+                lhsT_scale=operands[left][1][:],
+                rhs=operands[right][0][:].bitcast(FP8X4),
+                rhs_scale=operands[right][1][:],
+                start=start,
+                stop=not start,
+            )
+
+        def mm_x(i):
             acc = psum_acc.tile([P, D_ONE], F32)
-            nc.tensor.matmul_mx(
-                out=acc[:],
-                lhsT=x_codes[:].bitcast(FP8X4),
-                lhsT_scale=x_scales[:],
-                rhs=w1_codes[:].bitcast(FP8X4),
-                rhs_scale=w1_scales[:],
-                start=True,
-                stop=False,
-            )
-            nc.tensor.matmul_mx(
-                out=acc[:],
-                lhsT=g_codes[:].bitcast(FP8X4),
-                lhsT_scale=g_scales[:],
-                rhs=wg_codes[:].bitcast(FP8X4),
-                rhs_scale=wg_scales[:],
-                start=False,
-                stop=True,
-            )
-            accs.append(acc)
+            accs[i] = acc
+            mx(acc, "x%d" % i, "w1", True)
 
-        out_rows = out.rearrange("(g i) f -> g i f", i=NSPIN)
-        pre = keep.tile([P, NSPIN, D_ONE], F32)
-        th = keep.tile([P, NSPIN, D_ONE], F32)
-        res = keep.tile([P, NSPIN, D_ONE], F32)
-        for i in range(NSPIN + LAG):
-            if i < NSPIN:
-                nc.vector.tensor_tensor(out=pre[:, i, :], in0=accs[i][:], in1=bias_bc[:], op=ADD)
-                nc.scalar.activation(out=th[:, i, :], in_=pre[:, i, :], func=ACT.Tanh, scale=INV_SQRT2)
-            if i >= LAG:
-                j = i - LAG
-                nc.vector.scalar_tensor_tensor(
-                    out=res[:, j, :], in0=th[:, j, :], scalar=TANH_GAIN * INV_SQRT2, in1=h_res[:, j, :], op0=MULT, op1=ADD
-                )
-                nc.sync.dma_start(out=out_rows[:, j, :], in_=res[:, j, :])
+        def mm_g(i):
+            mx(accs[i], "g", "wg", False)
+
+        def add(i):
+            nc.vector.tensor_tensor(out=pre[:, i, :], in0=accs[i][:], in1=bias_bc[:], op=ADD)
+
+        def tanh(i):
+            nc.scalar.activation(out=th[:, i, :], in_=pre[:, i, :], func=ACT.Tanh, scale=INV_SQRT2)
+
+        def fin(i):
+            nc.vector.scalar_tensor_tensor(
+                out=res[:, i, :], in0=th[:, i, :], scalar=TANH_GAIN * INV_SQRT2, in1=h_res[:, i, :], op0=MULT, op1=ADD
+            )
+            nc.sync.dma_start(out=out_rows[:, i, :], in_=res[:, i, :])
+
+
+        s1(0)
+        s1(1)
+        s2(0)
+        xt(0)
+        residual_term()
+        xc(0)
+        s1(2)
+        s2(1)
+        xt(1)
+        w1_regroup()
+        xc(1)
+        s1(3)
+        q_x(0)
+        g_sums()
+        g_copy_own()
+        s2(2)
+        xt(2)
+        g_copy_other()
+        s2(3)
+        xt(3)
+        bias()
+        xc(2)
+        xc(3)
+        q_w1()
+        q_x(1)
+        wg_regroup(nc.vector.tensor_copy)
+        mm_x(0)
+        mm_x(1)
+        q_g()
+        q_wg()
+        q_x(2)
+        mm_g(0)
+        mm_x(2)
+        mm_g(1)
+        q_x(3)
+        add(0)
+        tanh(0)
+        mm_g(2)
+        add(1)
+        tanh(1)
+        mm_x(3)
+        mm_g(3)
+        add(2)
+        tanh(2)
+        fin(0)
+        add(3)
+        tanh(3)
+        fin(1)
+        fin(2)
+        fin(3)

@@ -29,14 +29,13 @@ def tile_fermilayer_pa_s_kernel(tc, h_one, h_two_same, h_two_diff, W1, b1, Wg, o
     nc = tc.nc
     with ExitStack() as ctx:
         keep = ctx.enter_context(tc.tile_pool(name="keep", bufs=1))
-        psum_t = ctx.enter_context(tc.psum_pool(name="psum_t", bufs=2))
+        psum_x = ctx.enter_context(tc.psum_pool(name="psum_x", bufs=4))
         psum_g = ctx.enter_context(tc.psum_pool(name="psum_g", bufs=1))
-        psum_acc = ctx.enter_context(tc.psum_pool(name="psum_acc", bufs=NSPIN))
+        psum_acc = ctx.enter_context(tc.psum_pool(name="psum_acc", bufs=3))
         ctx.enter_context(tc.manual_schedule())
 
         pair_rows = keep.tile([P, 2, NSPIN, NSPIN * D_TWO], BF16)
         rows = keep.tile([P, NSPIN, K], BF16)
-        h_nat = keep.tile([P, NSPIN, D_ONE], BF16)
         w1_raw = keep.tile([P, PACK, D_ONE], BF16)
         wg_raw = keep.tile([P, PACK, D_ONE], BF16)
         bias_row = keep.tile([P, D_ONE], BF16)
@@ -44,14 +43,11 @@ def tile_fermilayer_pa_s_kernel(tc, h_one, h_two_same, h_two_diff, W1, b1, Wg, o
             s.rearrange("(g i r) d -> g i (r d)", i=NSPIN, r=NSPIN) for s in (h_two_same, h_two_diff)
         ]
 
-        def load_pair(u, i):
-            nc.sync.dma_start(out=pair_rows[:, u, i, :], in_=streams[u][:, i, :])
+        def load_pair(u, a, b):
+            nc.sync.dma_start(out=pair_rows[:, u, a:b, :], in_=streams[u][:, a:b, :])
 
         def load_h():
             nc.sync.dma_start(out=rows[:, :, 0:D_ONE], in_=h_one.rearrange("(g i) k -> g i k", i=NSPIN))
-
-        def load_h_nat():
-            nc.sync.dma_start(out=h_nat[:], in_=h_one.rearrange("(r q) k -> q r k", q=P))
 
         def load_w1():
             nc.sync.dma_start(out=w1_raw[:], in_=W1.rearrange("(p t) n -> p t n", t=PACK))
@@ -70,33 +66,32 @@ def tile_fermilayer_pa_s_kernel(tc, h_one, h_two_same, h_two_diff, W1, b1, Wg, o
         mean_scale = keep.tile([P, 1], F32)
         nc.vector.memset(mean_scale[0 : P // 2], 1.0)
         nc.vector.memset(mean_scale[P // 2 : P], 1.0 / NSPIN)
-        load_pair(0, 0)
-        load_pair(1, 0)
-        load_pair(0, 1)
-        load_pair(1, 1)
+        load_pair(0, 0, 1)
+        load_pair(1, 0, 1)
+        load_pair(0, 1, 2)
+        load_pair(1, 1, 2)
         load_h()
-        load_pair(0, 2)
-        load_pair(1, 2)
+        load_pair(0, 2, 4)
         load_w1()
-        load_pair(0, 3)
-        load_pair(1, 3)
-        load_h_nat()
+        load_pair(1, 2, 4)
         load_wg()
-        nc.sync.dma_start(out=bias_row[0:1, :], in_=b1.rearrange("(o n) -> o n", o=1))
+        nc.scalar.dma_start(out=bias_row[0:1, :], in_=b1.rearrange("(o n) -> o n", o=1))
         nc.scalar.activation(out=warm[:], in_=warm[:], func=ACT.Tanh)
         ident = keep.tile([P, P], F32)
         make_identity(nc, ident[:])
-        sum_groups = keep.tile([P, P // NSPIN], BF16)
-        with nc.allow_low_precision(reason="sums of one 1 and zeros"):
-            nc.vector.tensor_reduce(
-                out=sum_groups[:], in_=ident[:].rearrange("q (g i) -> q g i", i=NSPIN), axis=mybir.AxisListType.X, op=ADD
-            )
+        swap = keep.tile([P, P], F32)
+        ident_ms = ident[:].rearrange("p (m s) -> p m s", s=2)
+        swap_ms = swap[:].rearrange("p (m s) -> p m s", s=2)
+        nc.gpsimd.tensor_copy(out=swap_ms[:, :, 0], in_=ident_ms[:, :, 1])
+        nc.gpsimd.tensor_copy(out=swap_ms[:, :, 1], in_=ident_ms[:, :, 0])
 
         x_grouped = keep.tile([P, NSPIN, P, PACK], BF16, align_bytes=64)
         g_grouped = keep.tile([P, P, PACK], BF16, align_bytes=64)
         w1_grouped = keep.tile([P, D_ONE, PACK], BF16, align_bytes=64)
         wg_grouped = keep.tile([P, D_ONE, PACK], BF16, align_bytes=64)
-        pair_half = keep.tile([P, NSPIN, 2, 2, D_TWO], F32)
+        pair_half = keep.tile([P, 2, NSPIN, 2, D_TWO], F32)
+        g_half = keep.tile([P, 2, D_ONE], F32)
+        g_sum = keep.tile([P, D_ONE], BF16)
         bias_bc = keep.tile([P, D_ONE], F32)
         h_res = keep.tile([P, NSPIN, D_ONE], F32)
         pre = keep.tile([P, NSPIN, D_ONE], F32)
@@ -105,81 +100,60 @@ def tile_fermilayer_pa_s_kernel(tc, h_one, h_two_same, h_two_diff, W1, b1, Wg, o
         out_rows = out.rearrange("(g i) f -> g i f", i=NSPIN)
         x_ts, accs, operands = {}, {}, {}
 
-        def s1(i):
-            four = pair_rows[:, :, i, :].rearrange("p u (a b d) -> p u a b d", a=2, b=2)
+        def s1(u, a, b):
+            four = pair_rows[:, u, a:b, :].rearrange("p i (a b d) -> p i a b d", a=2, b=2)
             nc.vector.tensor_tensor(
-                out=pair_half[:, i, :, :, :], in0=four[:, :, :, 0, :], in1=four[:, :, :, 1, :], op=ADD
+                out=pair_half[:, u, a:b, :, :], in0=four[:, :, :, 0, :], in1=four[:, :, :, 1, :], op=ADD
             )
 
         def s2(i):
             nc.vector.tensor_tensor(
-                out=rows[:, i, D_ONE:K].rearrange("p (u d) -> p u d", u=2),
-                in0=pair_half[:, i, :, 0, :],
-                in1=pair_half[:, i, :, 1, :],
-                op=ADD,
+                out=rows[:, i, D_ONE:K].rearrange("p (u d) -> p u d", u=2), in0=pair_half[:, :, i, 0, :], in1=pair_half[:, :, i, 1, :], op=ADD
             )
 
         def xt(i):
-            words = rows[:, i, :].bitcast(F32).rearrange("g (p u) -> g p u", u=2)
-            x_t = psum_t.tile([P, 2, P], F32)
+            row_words = rows[:, i, :].bitcast(F32).rearrange("g (p u) -> g p u", u=2)
+            x_t = psum_x.tile([P, 2, P], F32)
             for u in range(2):
-                nc.tensor.transpose(x_t[:, u, :], words[:, :, u], ident[:])
+                nc.tensor.transpose(x_t[:, u, :], row_words[:, :, u], ident[:])
             x_ts[i] = x_t
 
+        def words(grouped):
+            return grouped.rearrange("p g t -> p (g t)").bitcast(F32).rearrange("p (g u) -> p g u", u=2)
+
         def xc(i, copy=nc.scalar.copy):
-            copy(
-                out=x_grouped[:, i, :, :].rearrange("p g t -> p (g t)").bitcast(F32).rearrange("p (g u) -> p g u", u=2),
-                in_=x_ts[i][:].rearrange("p u g -> p g u"),
-            )
+            copy(out=words(x_grouped[:, i, :, :]), in_=x_ts[i][:].rearrange("p u g -> p g u"))
 
-        def g_sums():
+        def gs1():
+            nc.vector.tensor_tensor(out=g_half[:], in0=rows[:, 0:2, 0:D_ONE], in1=rows[:, 2:4, 0:D_ONE], op=ADD)
+
+        def gs2():
+            nc.vector.tensor_tensor(out=g_sum[:], in0=g_half[:, 0, :], in1=g_half[:, 1, :], op=ADD)
+
+        def gt():
             g_t = psum_g.tile([P, 2, P], F32)
+            nc.tensor.transpose(g_t[:, 0, :], g_sum[:].bitcast(F32), ident[:])
+            nc.tensor.transpose(g_t[:, 1, :], g_sum[:].bitcast(F32), swap[:])
             x_ts["g"] = g_t
-            for e in range(2):
-                for r in range(NSPIN):
-                    cols = slice(r * P // NSPIN, (r + 1) * P // NSPIN)
-                    nc.tensor.matmul(
-                        out=g_t[:, e, cols],
-                        lhsT=h_nat[:, r, :].rearrange("q (c e) -> q c e", e=2)[:, :, e],
-                        rhs=sum_groups[:],
-                        start=True,
-                        stop=True,
-                    )
 
-        def g_copy_own():
-            nc.scalar.activation(
-                out=g_grouped[:, :, 0:2], in_=x_ts["g"][:].rearrange("p e g -> p g e"), func=ACT.Copy, scale=1.0 / NSPIN
-            )
-
-        def g_copy_other():
-            nc.scalar.activation(
-                out=g_grouped[:, :, 2:4].rearrange("p (m s) e -> p m s e", s=2),
-                in_=x_ts["g"][:].rearrange("p e (m s) -> p m s e", s=2)[:, :, ::-1, :],
-                func=ACT.Copy,
-                scale=1.0 / NSPIN,
-            )
+        def gc():
+            nc.scalar.copy(out=words(g_grouped[:]), in_=x_ts["g"][:].rearrange("p o g -> p g o"))
 
         def bias():
-            bias_ps = psum_g.tile([P, D_ONE], F32)
+            bias_ps = psum_acc.tile([P, D_ONE], F32, name="acc")
             nc.tensor.matmul(out=bias_ps[:], lhsT=ones[:], rhs=bias_row[:], start=True, stop=True)
             nc.scalar.copy(out=bias_bc[:], in_=bias_ps[:])
 
-        def w1_regroup():
-            nc.scalar.activation(
-                out=w1_grouped[:].rearrange("p (c i) t -> p c t i", i=4),
-                in_=w1_raw[:].rearrange("p t (c i) -> p c t i", i=4),
-                func=ACT.Copy,
-                scale=mean_scale[:, 0:1],
-            )
+        def regroup(engine, grouped, raw, a, b, scale):
+            out_ = grouped[:, a:b, :].rearrange("p (c i) t -> p c t i", i=4)
+            in_ = raw[:, :, a:b].rearrange("p t (c i) -> p c t i", i=4)
+            if engine == "scalar":
+                nc.scalar.activation(out=out_, in_=in_, func=ACT.Copy, scale=scale)
+            else:
+                nc.vector.tensor_scalar(out=out_, in0=in_, scalar1=scale, scalar2=None, op0=MULT)
 
-        def wg_regroup(copy):
-            copy(
-                out=wg_grouped[:].rearrange("p (c i) t -> p c t i", i=4),
-                in_=wg_raw[:].rearrange("p t (c i) -> p c t i", i=4),
-            )
-
-        def residual_term():
-            nc.scalar.activation(out=h_res[:], in_=rows[:, :, 0:D_ONE], func=ACT.Copy, scale=INV_SQRT2)
+        def residual_term(a, b):
+            nc.scalar.activation(out=h_res[:, a:b, :], in_=rows[:, a:b, 0:D_ONE], func=ACT.Copy, scale=INV_SQRT2)
 
         def quantise(name, grouped, width):
             codes = keep.tile([P, width], U32, align_bytes=64, name=name + "_codes")
@@ -211,7 +185,7 @@ def tile_fermilayer_pa_s_kernel(tc, h_one, h_two_same, h_two_diff, W1, b1, Wg, o
             )
 
         def mm_x(i):
-            acc = psum_acc.tile([P, D_ONE], F32)
+            acc = psum_acc.tile([P, D_ONE], F32, name="acc")
             accs[i] = acc
             mx(acc, "x%d" % i, "w1", True)
 
@@ -230,49 +204,53 @@ def tile_fermilayer_pa_s_kernel(tc, h_one, h_two_same, h_two_diff, W1, b1, Wg, o
             )
             nc.sync.dma_start(out=out_rows[:, i, :], in_=res[:, i, :])
 
-
-        s1(0)
-        s1(1)
+        s1(0, 0, 1)
+        s1(1, 0, 1)
+        s1(0, 1, 2)
         s2(0)
+        s1(1, 1, 2)
+        residual_term(0, 2)
         xt(0)
-        residual_term()
-        xc(0)
-        s1(2)
+        gs1()
         s2(1)
+        xc(0)
+        bias()
         xt(1)
-        w1_regroup()
-        xc(1)
-        s1(3)
+        regroup("scalar", w1_grouped, w1_raw, 0, D_ONE, mean_scale[:, 0:1])
+        s1(0, 2, 4)
+        gs2()
+        gt()
+        s1(1, 2, 4)
         q_x(0)
-        g_sums()
-        g_copy_own()
+        xc(1)
+        gc()
         s2(2)
         xt(2)
-        g_copy_other()
         s2(3)
         xt(3)
-        bias()
+        regroup("scalar", wg_grouped, wg_raw, 0, P, 1.0 / NSPIN)
+        regroup("vector", wg_grouped, wg_raw, P, D_ONE, 1.0 / NSPIN)
         xc(2)
         xc(3)
         q_w1()
-        q_x(1)
-        wg_regroup(nc.vector.tensor_copy)
-        mm_x(0)
-        mm_x(1)
         q_g()
         q_wg()
-        q_x(2)
+        q_x(1)
+        mm_x(0)
         mm_g(0)
-        mm_x(2)
+        mm_x(1)
         mm_g(1)
+        residual_term(2, 4)
+        q_x(2)
+        mm_x(2)
+        mm_g(2)
         q_x(3)
         add(0)
         tanh(0)
-        mm_g(2)
-        add(1)
-        tanh(1)
         mm_x(3)
         mm_g(3)
+        add(1)
+        tanh(1)
         add(2)
         tanh(2)
         fin(0)

@@ -29,12 +29,13 @@ def tile_fermilayer_pa_s_kernel(tc, h_one, h_two_same, h_two_diff, W1, b1, Wg, o
     nc = tc.nc
     with ExitStack() as ctx:
         keep = ctx.enter_context(tc.tile_pool(name="keep", bufs=1))
-        psum_x = ctx.enter_context(tc.psum_pool(name="psum_x", bufs=4))
+        psum_x = ctx.enter_context(tc.psum_pool(name="psum_x", bufs=3))
         psum_g = ctx.enter_context(tc.psum_pool(name="psum_g", bufs=1))
-        psum_acc = ctx.enter_context(tc.psum_pool(name="psum_acc", bufs=3))
+        psum_acc = ctx.enter_context(tc.psum_pool(name="psum_acc", bufs=4))
         ctx.enter_context(tc.manual_schedule())
 
         pair_rows = keep.tile([P, 2, NSPIN, NSPIN * D_TWO], BF16)
+        h_rows = keep.tile([P, NSPIN, D_ONE], BF16)
         rows = keep.tile([P, NSPIN, K], BF16)
         w1_raw = keep.tile([P, PACK, D_ONE], BF16)
         wg_raw = keep.tile([P, PACK, D_ONE], BF16)
@@ -47,7 +48,7 @@ def tile_fermilayer_pa_s_kernel(tc, h_one, h_two_same, h_two_diff, W1, b1, Wg, o
             nc.sync.dma_start(out=pair_rows[:, u, a:b, :], in_=streams[u][:, a:b, :])
 
         def load_h():
-            nc.sync.dma_start(out=rows[:, :, 0:D_ONE], in_=h_one.rearrange("(g i) k -> g i k", i=NSPIN))
+            nc.sync.dma_start(out=h_rows[:], in_=h_one.rearrange("(g i) k -> g i k", i=NSPIN))
 
         def load_w1():
             nc.sync.dma_start(out=w1_raw[:], in_=W1.rearrange("(p t) n -> p t n", t=PACK))
@@ -66,11 +67,9 @@ def tile_fermilayer_pa_s_kernel(tc, h_one, h_two_same, h_two_diff, W1, b1, Wg, o
         mean_scale = keep.tile([P, 1], F32)
         nc.vector.memset(mean_scale[0 : P // 2], 1.0)
         nc.vector.memset(mean_scale[P // 2 : P], 1.0 / NSPIN)
-        load_pair(0, 0, 1)
-        load_pair(1, 0, 1)
-        load_pair(0, 1, 2)
-        load_pair(1, 1, 2)
         load_h()
+        load_pair(0, 0, 2)
+        load_pair(1, 0, 2)
         load_pair(0, 2, 4)
         load_w1()
         load_pair(1, 2, 4)
@@ -111,6 +110,9 @@ def tile_fermilayer_pa_s_kernel(tc, h_one, h_two_same, h_two_diff, W1, b1, Wg, o
                 out=rows[:, i, D_ONE:K].rearrange("p (u d) -> p u d", u=2), in0=pair_half[:, :, i, 0, :], in1=pair_half[:, :, i, 1, :], op=ADD
             )
 
+        def hcw(a, b):
+            nc.scalar.copy(out=rows[:].bitcast(F32)[:, a:b, 0 : D_ONE // 2], in_=h_rows[:].bitcast(F32)[:, a:b, :])
+
         def xt(i):
             row_words = rows[:, i, :].bitcast(F32).rearrange("g (p u) -> g p u", u=2)
             x_t = psum_x.tile([P, 2, P], F32)
@@ -125,7 +127,7 @@ def tile_fermilayer_pa_s_kernel(tc, h_one, h_two_same, h_two_diff, W1, b1, Wg, o
             copy(out=words(x_grouped[:, i, :, :]), in_=x_ts[i][:].rearrange("p u g -> p g u"))
 
         def gs1():
-            nc.vector.tensor_tensor(out=g_half[:], in0=rows[:, 0:2, 0:D_ONE], in1=rows[:, 2:4, 0:D_ONE], op=ADD)
+            nc.vector.tensor_tensor(out=g_half[:], in0=h_rows[:, 0:2, :], in1=h_rows[:, 2:4, :], op=ADD)
 
         def gs2():
             nc.vector.tensor_tensor(out=g_sum[:], in0=g_half[:, 0, :], in1=g_half[:, 1, :], op=ADD)
@@ -153,7 +155,7 @@ def tile_fermilayer_pa_s_kernel(tc, h_one, h_two_same, h_two_diff, W1, b1, Wg, o
                 nc.vector.tensor_scalar(out=out_, in0=in_, scalar1=scale, scalar2=None, op0=MULT)
 
         def residual_term(a, b):
-            nc.scalar.activation(out=h_res[:, a:b, :], in_=rows[:, a:b, 0:D_ONE], func=ACT.Copy, scale=INV_SQRT2)
+            nc.scalar.activation(out=h_res[:, a:b, :], in_=h_rows[:, a:b, :], func=ACT.Copy, scale=INV_SQRT2)
 
         def quantise(name, grouped, width):
             codes = keep.tile([P, width], U32, align_bytes=64, name=name + "_codes")
@@ -204,51 +206,51 @@ def tile_fermilayer_pa_s_kernel(tc, h_one, h_two_same, h_two_diff, W1, b1, Wg, o
             )
             nc.sync.dma_start(out=out_rows[:, i, :], in_=res[:, i, :])
 
-        s1(0, 0, 1)
-        s1(1, 0, 1)
-        s1(0, 1, 2)
-        s2(0)
-        s1(1, 1, 2)
+        hcw(0, 2)
+        hcw(2, 4)
         residual_term(0, 2)
-        xt(0)
-        gs1()
-        s2(1)
-        xc(0)
+        residual_term(2, 4)
         bias()
-        xt(1)
-        regroup("scalar", w1_grouped, w1_raw, 0, D_ONE, mean_scale[:, 0:1])
-        s1(0, 2, 4)
+        gs1()
+        s1(0, 0, 2)
         gs2()
         gt()
-        s1(1, 2, 4)
-        q_x(0)
-        xc(1)
         gc()
+        s1(1, 0, 2)
+        s1(0, 2, 4)
+        s2(0)
+        xt(0)
+        s2(1)
+        xt(1)
+        regroup("scalar", w1_grouped, w1_raw, 0, D_ONE, mean_scale[:, 0:1])
+        s1(1, 2, 4)
+        q_g()
         s2(2)
         xt(2)
         s2(3)
         xt(3)
-        regroup("scalar", wg_grouped, wg_raw, 0, P, 1.0 / NSPIN)
-        regroup("vector", wg_grouped, wg_raw, P, D_ONE, 1.0 / NSPIN)
+        xc(0)
+        regroup("vector", wg_grouped, wg_raw, 192, D_ONE, 1.0 / NSPIN)
+        regroup("scalar", wg_grouped, wg_raw, 0, 192, 1.0 / NSPIN)
+        xc(1)
         xc(2)
         xc(3)
         q_w1()
-        q_g()
-        q_wg()
-        q_x(1)
+        q_x(0)
         mm_x(0)
+        q_wg()
         mm_g(0)
+        q_x(1)
         mm_x(1)
         mm_g(1)
-        residual_term(2, 4)
         q_x(2)
         mm_x(2)
         mm_g(2)
         q_x(3)
-        add(0)
-        tanh(0)
         mm_x(3)
         mm_g(3)
+        add(0)
+        tanh(0)
         add(1)
         tanh(1)
         add(2)

@@ -69,12 +69,12 @@ def tile_fermilayer_pa_s_kernel(tc, h_one, h_two_same, h_two_diff, W1, b1, Wg, o
         nc.vector.memset(mean_scale[P // 2 : P], 1.0 / NSPIN)
         load_h()
         load_pair(0, 0, 2)
+        nc.sync.dma_start(out=bias_row[0:1, :], in_=b1.rearrange("(o n) -> o n", o=1))
         load_pair(1, 0, 2)
         load_pair(0, 2, 4)
         load_w1()
         load_pair(1, 2, 4)
         load_wg()
-        nc.scalar.dma_start(out=bias_row[0:1, :], in_=b1.rearrange("(o n) -> o n", o=1))
         nc.scalar.activation(out=warm[:], in_=warm[:], func=ACT.Tanh)
         ident = keep.tile([P, P], F32)
         make_identity(nc, ident[:])
@@ -230,8 +230,8 @@ def tile_fermilayer_pa_s_kernel(tc, h_one, h_two_same, h_two_diff, W1, b1, Wg, o
         s2(3)
         xt(3)
         xc(0)
-        regroup("vector", wg_grouped, wg_raw, 192, D_ONE, 1.0 / NSPIN)
-        regroup("scalar", wg_grouped, wg_raw, 0, 192, 1.0 / NSPIN)
+        regroup("vector", wg_grouped, wg_raw, P, D_ONE, 1.0 / NSPIN)
+        regroup("scalar", wg_grouped, wg_raw, 0, P, 1.0 / NSPIN)
         xc(1)
         xc(2)
         xc(3)

@@ -61,12 +61,9 @@ def tile_fermilayer_pa_s_kernel(tc, h_one, h_two_same, h_two_diff, W1, b1, Wg, o
 
         nc.vector.memset(bias_row[:], 0.0)
         ones = keep.tile([P, P], BF16)
-        nc.vector.memset(ones[:], 1.0)
+        nc.vector.memset(ones[:], 1.0 * NSPIN)
         warm = keep.tile([P, 1], F32)
         nc.vector.memset(warm[:], 0.0)
-        mean_scale = keep.tile([P, 1], F32)
-        nc.vector.memset(mean_scale[0 : P // 2], 1.0)
-        nc.vector.memset(mean_scale[P // 2 : P], 1.0 / NSPIN)
         load_h()
         load_pair(0, 0, 2)
         nc.sync.dma_start(out=bias_row[0:1, :], in_=b1.rearrange("(o n) -> o n", o=1))
@@ -111,7 +108,7 @@ def tile_fermilayer_pa_s_kernel(tc, h_one, h_two_same, h_two_diff, W1, b1, Wg, o
             )
 
         def hcw(a, b):
-            nc.scalar.copy(out=rows[:].bitcast(F32)[:, a:b, 0 : D_ONE // 2], in_=h_rows[:].bitcast(F32)[:, a:b, :])
+            nc.scalar.activation(out=rows[:, a:b, 0:D_ONE], in_=h_rows[:, a:b, :], func=ACT.Copy, scale=1.0 * NSPIN)
 
         def xt(i):
             row_words = rows[:, i, :].bitcast(F32).rearrange("g (p u) -> g p u", u=2)
@@ -146,13 +143,10 @@ def tile_fermilayer_pa_s_kernel(tc, h_one, h_two_same, h_two_diff, W1, b1, Wg, o
             nc.tensor.matmul(out=bias_ps[:], lhsT=ones[:], rhs=bias_row[:], start=True, stop=True)
             nc.scalar.copy(out=bias_bc[:], in_=bias_ps[:])
 
-        def regroup(engine, grouped, raw, a, b, scale):
+        def regroup(engine, grouped, raw, a, b):
             out_ = grouped[:, a:b, :].rearrange("p (c i) t -> p c t i", i=4)
             in_ = raw[:, :, a:b].rearrange("p t (c i) -> p c t i", i=4)
-            if engine == "scalar":
-                nc.scalar.activation(out=out_, in_=in_, func=ACT.Copy, scale=scale)
-            else:
-                nc.vector.tensor_scalar(out=out_, in0=in_, scalar1=scale, scalar2=None, op0=MULT)
+            (nc.scalar.copy if engine == "scalar" else nc.vector.tensor_copy)(out=out_, in_=in_)
 
         def residual_term(a, b):
             nc.scalar.activation(out=h_res[:, a:b, :], in_=h_rows[:, a:b, :], func=ACT.Copy, scale=INV_SQRT2)
@@ -198,7 +192,7 @@ def tile_fermilayer_pa_s_kernel(tc, h_one, h_two_same, h_two_diff, W1, b1, Wg, o
             nc.vector.tensor_tensor(out=pre[:, i, :], in0=accs[i][:], in1=bias_bc[:], op=ADD)
 
         def tanh(i):
-            nc.scalar.activation(out=th[:, i, :], in_=pre[:, i, :], func=ACT.Tanh, scale=INV_SQRT2)
+            nc.scalar.activation(out=th[:, i, :], in_=pre[:, i, :], func=ACT.Tanh, scale=INV_SQRT2 / NSPIN)
 
         def fin(i):
             nc.vector.scalar_tensor_tensor(
@@ -209,7 +203,6 @@ def tile_fermilayer_pa_s_kernel(tc, h_one, h_two_same, h_two_diff, W1, b1, Wg, o
         hcw(0, 2)
         hcw(2, 4)
         residual_term(0, 2)
-        residual_term(2, 4)
         bias()
         gs1()
         s1(0, 0, 2)
@@ -222,7 +215,7 @@ def tile_fermilayer_pa_s_kernel(tc, h_one, h_two_same, h_two_diff, W1, b1, Wg, o
         xt(0)
         s2(1)
         xt(1)
-        regroup("scalar", w1_grouped, w1_raw, 0, D_ONE, mean_scale[:, 0:1])
+        regroup("scalar", w1_grouped, w1_raw, 0, D_ONE)
         s1(1, 2, 4)
         q_g()
         s2(2)
@@ -230,11 +223,12 @@ def tile_fermilayer_pa_s_kernel(tc, h_one, h_two_same, h_two_diff, W1, b1, Wg, o
         s2(3)
         xt(3)
         xc(0)
-        regroup("vector", wg_grouped, wg_raw, P, D_ONE, 1.0 / NSPIN)
-        regroup("scalar", wg_grouped, wg_raw, 0, P, 1.0 / NSPIN)
+        regroup("vector", wg_grouped, wg_raw, P, D_ONE)
+        regroup("scalar", wg_grouped, wg_raw, 0, P)
         xc(1)
         xc(2)
         xc(3)
+        residual_term(2, 4)
         q_w1()
         q_x(0)
         mm_x(0)

@@ -36,7 +36,7 @@ def tile_fermilayer_pa_s_kernel(tc, h_one, h_two_same, h_two_diff, W1, b1, Wg, o
 
         pair_rows = keep.tile([P, 2, NSPIN, NSPIN * D_TWO], BF16)
         h_rows = keep.tile([P, NSPIN, D_ONE], BF16)
-        rows = keep.tile([P, NSPIN, K], BF16)
+        rows = keep.tile([P, NSPIN, 2, P, 2], BF16)
         w1_raw = keep.tile([P, PACK, D_ONE], BF16)
         wg_raw = keep.tile([P, PACK, D_ONE], BF16)
         bias_row = keep.tile([P, D_ONE], BF16)
@@ -85,7 +85,7 @@ def tile_fermilayer_pa_s_kernel(tc, h_one, h_two_same, h_two_diff, W1, b1, Wg, o
         g_grouped = keep.tile([P, P, PACK], BF16, align_bytes=64)
         w1_grouped = keep.tile([P, D_ONE, PACK], BF16, align_bytes=64)
         wg_grouped = keep.tile([P, D_ONE, PACK], BF16, align_bytes=64)
-        pair_half = keep.tile([P, 2, NSPIN, 2, D_TWO], F32)
+        pair_half = keep.tile([P, NSPIN, 2, 2, D_TWO], F32)
         g_half = keep.tile([P, 2, D_ONE], F32)
         g_sum = keep.tile([P, D_ONE], BF16)
         bias_bc = keep.tile([P, D_ONE], F32)
@@ -99,22 +99,30 @@ def tile_fermilayer_pa_s_kernel(tc, h_one, h_two_same, h_two_diff, W1, b1, Wg, o
         def s1(u, a, b):
             four = pair_rows[:, u, a:b, :].rearrange("p i (a b d) -> p i a b d", a=2, b=2)
             nc.vector.tensor_tensor(
-                out=pair_half[:, u, a:b, :, :], in0=four[:, :, :, 0, :], in1=four[:, :, :, 1, :], op=ADD
+                out=pair_half[:, a:b, :, u, :], in0=four[:, :, :, 0, :], in1=four[:, :, :, 1, :], op=ADD
             )
 
         def s2(i):
             nc.vector.tensor_tensor(
-                out=rows[:, i, D_ONE:K].rearrange("p (u d) -> p u d", u=2), in0=pair_half[:, :, i, 0, :], in1=pair_half[:, :, i, 1, :], op=ADD
+
+                out=rows[:, i, :, P // 2 :, :],
+                in0=pair_half[:, i, 0, :, :].rearrange("g s (q u e) -> g u (s q) e", u=2, e=2),
+                in1=pair_half[:, i, 1, :, :].rearrange("g s (q u e) -> g u (s q) e", u=2, e=2),
+                op=ADD,
             )
 
-        def hcw(a, b):
-            nc.scalar.activation(out=rows[:, a:b, 0:D_ONE], in_=h_rows[:, a:b, :], func=ACT.Copy, scale=1.0 * NSPIN)
+        def hcw(u):
+            nc.scalar.activation(
+                out=rows[:, :, u, 0 : P // 2, :],
+                in_=h_rows[:].rearrange("g i (p u e) -> g i u p e", u=2, e=2)[:, :, u, :, :],
+                func=ACT.Copy,
+                scale=1.0 * NSPIN,
+            )
 
         def xt(i):
-            row_words = rows[:, i, :].bitcast(F32).rearrange("g (p u) -> g p u", u=2)
             x_t = psum_x.tile([P, 2, P], F32)
             for u in range(2):
-                nc.tensor.transpose(x_t[:, u, :], row_words[:, :, u], ident[:])
+                nc.tensor.transpose(x_t[:, u, :], rows[:, i, u, :, :].rearrange("g p e -> g (p e)").bitcast(F32), ident[:])
             x_ts[i] = x_t
 
         def words(grouped):
@@ -200,8 +208,8 @@ def tile_fermilayer_pa_s_kernel(tc, h_one, h_two_same, h_two_diff, W1, b1, Wg, o
             )
             nc.sync.dma_start(out=out_rows[:, i, :], in_=res[:, i, :])
 
-        hcw(0, 2)
-        hcw(2, 4)
+        hcw(0)
+        hcw(1)
         residual_term(0, 2)
         bias()
         gs1()
@@ -223,8 +231,8 @@ def tile_fermilayer_pa_s_kernel(tc, h_one, h_two_same, h_two_diff, W1, b1, Wg, o
         s2(3)
         xt(3)
         xc(0)
-        regroup("vector", wg_grouped, wg_raw, P, D_ONE)
-        regroup("scalar", wg_grouped, wg_raw, 0, P)
+        regroup("vector", wg_grouped, wg_raw, 160, D_ONE)
+        regroup("scalar", wg_grouped, wg_raw, 0, 160)
         xc(1)
         xc(2)
         xc(3)

import math
from contextlib import ExitStack

import concourse.mybir as mybir
from concourse.masks import make_identity

BF16 = mybir.dt.bfloat16
F32 = mybir.dt.float32
U32 = mybir.dt.uint32
U8 = mybir.dt.uint8
FP8X4 = mybir.dt.float8_e4m3fn_x4
ADD = mybir.AluOpType.add
MULT = mybir.AluOpType.mult
ACT = mybir.ActivationFunctionType

P = 128
NSPIN = 4
D_ONE = 256
D_TWO = 128
K = 512
PACK = 4
TANH_GAIN = 1.5927812698663606
INV_SQRT2 = 1.0 / math.sqrt(2.0)

FLOPS = 2 * (P * NSPIN) * K * D_ONE + 2 * P * K * D_ONE


def tile_fermilayer_pa_s_kernel(tc, h_one, h_two_same, h_two_diff, W1, b1, Wg, out):
    nc = tc.nc
    with ExitStack() as ctx:
        keep = ctx.enter_context(tc.tile_pool(name="keep", bufs=1))
        psum_x = ctx.enter_context(tc.psum_pool(name="psum_x", bufs=3))
        psum_g = ctx.enter_context(tc.psum_pool(name="psum_g", bufs=1))
        psum_acc = ctx.enter_context(tc.psum_pool(name="psum_acc", bufs=4))
        ctx.enter_context(tc.manual_schedule())

        pair_rows = keep.tile([P, 2, NSPIN, NSPIN * D_TWO], BF16)
        h_rows = keep.tile([P, NSPIN, D_ONE], BF16)
        rows = keep.tile([P, NSPIN, 2, P, 2], BF16)
        w1_raw = keep.tile([P, PACK, D_ONE], BF16)
        wg_raw = keep.tile([P, PACK, D_ONE], BF16)
        bias_row = keep.tile([P, D_ONE], BF16)
        streams = [
            s.rearrange("(g i r) d -> g i (r d)", i=NSPIN, r=NSPIN) for s in (h_two_same, h_two_diff)
        ]

        def load_pair(u, a, b):
            nc.sync.dma_start(out=pair_rows[:, u, a:b, :], in_=streams[u][:, a:b, :])

        def load_h():
            nc.sync.dma_start(out=h_rows[:], in_=h_one.rearrange("(g i) k -> g i k", i=NSPIN))

        def load_w1():
            nc.sync.dma_start(out=w1_raw[:], in_=W1.rearrange("(p t) n -> p t n", t=PACK))

        def load_wg():
            nc.sync.dma_start(
                out=wg_raw[:].rearrange("p (o e) n -> p o (e n)", o=2),
                in_=Wg.rearrange("(o p e) n -> p o (e n)", o=2, e=2),
            )

        nc.vector.memset(bias_row[:], 0.0)
        ones = keep.tile([P, P], BF16)
        nc.vector.memset(ones[:], 1.0 * NSPIN)
        warm = keep.tile([P, 1], F32)
        nc.vector.memset(warm[:], 0.0)
        load_h()
        load_pair(0, 0, 2)
        nc.sync.dma_start(out=bias_row[0:1, :], in_=b1.rearrange("(o n) -> o n", o=1))
        load_pair(1, 0, 2)
        load_pair(0, 2, 4)
        load_w1()
        load_pair(1, 2, 4)
        load_wg()
        nc.scalar.activation(out=warm[:], in_=warm[:], func=ACT.Tanh)
        ident = keep.tile([P, P], F32)
        make_identity(nc, ident[:])
        swap = keep.tile([P, P], F32)
        ident_ms = ident[:].rearrange("p (m s) -> p m s", s=2)
        swap_ms = swap[:].rearrange("p (m s) -> p m s", s=2)
        nc.gpsimd.tensor_copy(out=swap_ms[:, :, 0], in_=ident_ms[:, :, 1])
        nc.gpsimd.tensor_copy(out=swap_ms[:, :, 1], in_=ident_ms[:, :, 0])

        x_grouped = keep.tile([P, NSPIN, P, PACK], BF16, align_bytes=64)
        g_grouped = keep.tile([P, P, PACK], BF16, align_bytes=64)
        w1_grouped = keep.tile([P, D_ONE, PACK], BF16, align_bytes=64)
        wg_grouped = keep.tile([P, D_ONE, PACK], BF16, align_bytes=64)
        pair_half = keep.tile([P, NSPIN, 2, 2, D_TWO], F32)
        g_half = keep.tile([P, 2, D_ONE], F32)
        g_sum = keep.tile([P, D_ONE], BF16)
        bias_bc = keep.tile([P, D_ONE], F32)
        h_res = keep.tile([P, NSPIN, D_ONE], F32)
        pre = keep.tile([P, NSPIN, D_ONE], F32)
        th = keep.tile([P, NSPIN, D_ONE], F32)
        res = keep.tile([P, NSPIN, D_ONE], F32)
        out_rows = out.rearrange("(g i) f -> g i f", i=NSPIN)
        x_ts, accs, operands = {}, {}, {}

        def s1(u, a, b):
            four = pair_rows[:, u, a:b, :].rearrange("p i (a b d) -> p i a b d", a=2, b=2)
            nc.vector.tensor_tensor(
                out=pair_half[:, a:b, :, u, :], in0=four[:, :, :, 0, :], in1=four[:, :, :, 1, :], op=ADD
            )

        def s2(i):
            nc.vector.tensor_tensor(

                out=rows[:, i, :, P // 2 :, :],
                in0=pair_half[:, i, 0, :, :].rearrange("g s (q u e) -> g u (s q) e", u=2, e=2),
                in1=pair_half[:, i, 1, :, :].rearrange("g s (q u e) -> g u (s q) e", u=2, e=2),
                op=ADD,
            )

        def hcw(u):
            nc.scalar.activation(
                out=rows[:, :, u, 0 : P // 2, :],
                in_=h_rows[:].rearrange("g i (p u e) -> g i u p e", u=2, e=2)[:, :, u, :, :],
                func=ACT.Copy,
                scale=1.0 * NSPIN,
            )

        def xt(i):
            x_t = psum_x.tile([P, 2, P], F32)
            for u in range(2):
                nc.tensor.transpose(x_t[:, u, :], rows[:, i, u, :, :].rearrange("g p e -> g (p e)").bitcast(F32), ident[:])
            x_ts[i] = x_t

        def words(grouped):
            return grouped.rearrange("p g t -> p (g t)").bitcast(F32).rearrange("p (g u) -> p g u", u=2)

        def xc(i, copy=nc.scalar.copy):
            copy(out=words(x_grouped[:, i, :, :]), in_=x_ts[i][:].rearrange("p u g -> p g u"))

        def gs1():
            nc.vector.tensor_tensor(out=g_half[:], in0=h_rows[:, 0:2, :], in1=h_rows[:, 2:4, :], op=ADD)

        def gs2():
            nc.vector.tensor_tensor(out=g_sum[:], in0=g_half[:, 0, :], in1=g_half[:, 1, :], op=ADD)

        def gt():
            g_t = psum_g.tile([P, 2, P], F32)
            nc.tensor.transpose(g_t[:, 0, :], g_sum[:].bitcast(F32), ident[:])
            nc.tensor.transpose(g_t[:, 1, :], g_sum[:].bitcast(F32), swap[:])
            x_ts["g"] = g_t

        def gc():
            nc.scalar.copy(out=words(g_grouped[:]), in_=x_ts["g"][:].rearrange("p o g -> p g o"))

        def bias():
            bias_ps = psum_acc.tile([P, D_ONE], F32, name="acc")
            nc.tensor.matmul(out=bias_ps[:], lhsT=ones[:], rhs=bias_row[:], start=True, stop=True)
            nc.scalar.copy(out=bias_bc[:], in_=bias_ps[:])

        def regroup(engine, grouped, raw, a, b):
            out_ = grouped[:, a:b, :].rearrange("p (c i) t -> p c t i", i=4)
            in_ = raw[:, :, a:b].rearrange("p t (c i) -> p c t i", i=4)
            (nc.scalar.copy if engine == "scalar" else nc.vector.tensor_copy)(out=out_, in_=in_)

        def residual_term(a, b):
            nc.scalar.activation(out=h_res[:, a:b, :], in_=h_rows[:, a:b, :], func=ACT.Copy, scale=INV_SQRT2)

        def quantise(name, grouped, width):
            codes = keep.tile([P, width], U32, align_bytes=64, name=name + "_codes")
            scales = keep.tile([P, width], U8, align_bytes=64, name=name + "_scales")
            nc.vector.quantize_mx(out=codes[:].bitcast(FP8X4), scales=scales[:], in_=grouped)
            operands[name] = codes, scales

        def q_w1():
            quantise("w1", w1_grouped[:].rearrange("p n t -> p (n t)"), D_ONE)

        def q_wg():
            quantise("wg", wg_grouped[:].rearrange("p n t -> p (n t)"), D_ONE)

        def q_g():
            quantise("g", g_grouped[:].rearrange("p g t -> p (g t)"), P)

        def q_x(i):
            quantise("x%d" % i, x_grouped[:, i, :, :].rearrange("p g t -> p (g t)"), P)

        def mx(acc, left, right, start):
            nc.tensor.matmul_mx(
                out=acc[:],
                lhsT=operands[left][0][:].bitcast(FP8X4),
                lhsT_scale=operands[left][1][:],
                rhs=operands[right][0][:].bitcast(FP8X4),
                rhs_scale=operands[right][1][:],
                start=start,
                stop=not start,
            )

        def mm_x(i):
            acc = psum_acc.tile([P, D_ONE], F32, name="acc")
            accs[i] = acc
            mx(acc, "x%d" % i, "w1", True)

        def mm_g(i):
            mx(accs[i], "g", "wg", False)

        def add(i):
            nc.vector.tensor_tensor(out=pre[:, i, :], in0=accs[i][:], in1=bias_bc[:], op=ADD)

        def tanh(i):
            nc.scalar.activation(out=th[:, i, :], in_=pre[:, i, :], func=ACT.Tanh, scale=INV_SQRT2 / NSPIN)

        def fin(i):
            nc.vector.scalar_tensor_tensor(
                out=res[:, i, :], in0=th[:, i, :], scalar=TANH_GAIN * INV_SQRT2, in1=h_res[:, i, :], op0=MULT, op1=ADD
            )
            nc.sync.dma_start(out=out_rows[:, i, :], in_=res[:, i, :])

        hcw(0)
        hcw(1)
        residual_term(0, 2)
        bias()
        gs1()
        s1(0, 0, 2)
        gs2()
        gt()
        gc()
        s1(1, 0, 2)
        s1(0, 2, 4)
        s2(0)
        xt(0)
        s2(1)
        xt(1)
        regroup("scalar", w1_grouped, w1_raw, 0, D_ONE)
        s1(1, 2, 4)
        q_g()
        s2(2)
        xt(2)
        s2(3)
        xt(3)
        xc(0)
        regroup("vector", wg_grouped, wg_raw, 160, D_ONE)
        regroup("scalar", wg_grouped, wg_raw, 0, 160)
        xc(1)
        xc(2)
        xc(3)
        residual_term(2, 4)
        q_w1()
        q_x(0)
        mm_x(0)
        q_wg()
        mm_g(0)
        q_x(1)
        mm_x(1)
        mm_g(1)
        q_x(2)
        mm_x(2)
        mm_g(2)
        q_x(3)
        mm_x(3)
        mm_g(3)
        add(0)
        tanh(0)
        add(1)
        tanh(1)
        add(2)
        tanh(2)
        fin(0)
        add(3)
        tanh(3)
        fin(1)
        fin(2)
        fin(3)
